import numpy as np
import ml_dtypes


def mxq(x, axis, fmt="e4m3"):
    dtype, down = {"e4m3": (ml_dtypes.float8_e4m3fn, 7), "e5m2": (ml_dtypes.float8_e5m2, 14)}[fmt]
    v = np.moveaxis(np.asarray(x, np.float32).astype(ml_dtypes.bfloat16).astype(np.float64), axis, -1)
    blocks = v.reshape(v.shape[:-1] + (-1, 32))
    amax = np.abs(blocks).max(-1, keepdims=True)
    byte = np.maximum(np.where(amax > 0, np.frexp(amax)[1] - 1 + 127, 0) - down, 1)
    scale = np.exp2(byte - 127.0)
    codes = (blocks / scale).astype(np.float32).astype(dtype).astype(np.float64)
    return np.moveaxis((codes * scale).reshape(v.shape), -1, axis)


WIDE = False


def mx_kscale(k):
    if not WIDE:
        return np.ones(k)
    levels = np.array([10, -10, 5, -5, 0])
    if k % 512:
        return np.exp2(np.random.permutation(np.resize(levels, k // 32))).repeat(32)
    a = np.empty((k // 512, 16))
    for p in range(k // 512):
        a[p, :8] = np.random.permutation(np.resize(levels, 8))
        for g in range(8):
            far = levels[np.abs(levels - a[p, g]) >= 10]
            a[p, g + 8] = far[np.random.randint(len(far))]
    return np.exp2(a.ravel()).repeat(32)


BF16 = ml_dtypes.bfloat16


def bf(x):
    return np.asarray(x, np.float32).astype(BF16)


def f64(x):
    return np.asarray(x).astype(np.float64)


B, R, U, HID, G = 256, 16384, 512, 1024, 256


def sigmoid(v):
    return 1.0 / (1.0 + np.exp(-v))


def setup_inputs():
    s = mx_kscale(R)
    return {"y_tilde": bf(np.random.standard_normal((B, R)) * s),
            "z_next": bf(np.random.standard_normal((B, R)) * s),
            "dt": bf(0.3 + 0.2 * np.random.random(1)),
            "glu_w1": bf(np.random.standard_normal((G, R)) * 1.5 / np.sqrt(R) / s),
            "glu_w2": bf(np.random.standard_normal((G, R)) / np.sqrt(R) / s),
            "glu_b1": bf(np.random.standard_normal(G) * 0.3),
            "glu_b2": bf(np.random.standard_normal(G) * 0.3)}


def reference(y_tilde, z_next, dt, glu_w1, glu_w2, glu_b1, glu_b2):
    y_next = f64(y_tilde) + f64(dt) * f64(z_next)
    yq = mxq(y_next, 1, "e4m3")
    gate = sigmoid((yq @ mxq(f64(glu_w1), 1, "e4m3").T) + f64(glu_b1))
    return gate * ((yq @ mxq(f64(glu_w2), 1, "e4m3").T) + f64(glu_b2))

@@ -1,0 +1,228 @@
+from contextlib import ExitStack
+
+import concourse.mybir as mybir
+from concourse.masks import make_identity
+
+BF16 = mybir.dt.bfloat16
+F32 = mybir.dt.float32
+U32 = mybir.dt.uint32
+U8 = mybir.dt.uint8
+FP8X4 = mybir.dt.float8_e4m3fn_x4
+ALU = mybir.AluOpType
+ACT = mybir.ActivationFunctionType
+
+BATCH, MODES, GATES = 256, 16384, 256
+
+P = 128
+PACK = 4
+K_PASS = P * PACK
+PASSES = MODES // K_PASS
+ROW_TILES = 2
+PAIR_HALVES = 2
+
+CHUNK_PASSES = 4
+CHUNK = CHUNK_PASSES * K_PASS
+CHUNKS = PASSES // CHUNK_PASSES
+HALF_PASSES = CHUNK_PASSES // 2
+HALF = HALF_PASSES * K_PASS
+
+BANKS_PER_PASS = 3
+
+N_OUT = 2 * GATES
+
+FLOPS = 2 * BATCH * MODES * N_OUT
+
+
+def tile_instrumentedlocmblock_pb_k_kernel(
+    tc, y_tilde, z_next, dt, glu_w1, glu_w2, glu_b1, glu_b2, out
+):
+    nc = tc.nc
+    with ExitStack() as ctx:
+        consts = ctx.enter_context(tc.tile_pool(name="consts", bufs=1))
+        loads = ctx.enter_context(tc.tile_pool(name="loads", bufs=3))
+        stage = ctx.enter_context(tc.tile_pool(name="stage", bufs=3))
+        finish = ctx.enter_context(tc.tile_pool(name="finish", bufs=2))
+        banks = ctx.enter_context(tc.psum_pool(name="banks", bufs=6))
+        sums = ctx.enter_context(tc.psum_pool(name="sums", bufs=1))
+        ctx.enter_context(tc.manual_schedule())
+
+        def load(src, c, name):
+            rows = loads.tile([P, ROW_TILES, CHUNK], BF16, name=name)
+            nc.sync.dma_start(
+                out=rows[:],
+                in_=src.rearrange("(a p) k -> p a k", p=P)[:, :, c * CHUNK : (c + 1) * CHUNK],
+            )
+            return rows
+
+        y_rows, z_rows, w1_rows, w2_rows = {}, {}, {}, {}
+
+        def load_positions(c):
+            y_rows[c] = load(y_tilde, c, "y_rows")
+            z_rows[c] = load(z_next, c, "z_rows")
+
+        def load_weights(c):
+            w1_rows[c] = load(glu_w1, c, "w1_rows")
+            w2_rows[c] = load(glu_w2, c, "w2_rows")
+
+        load_positions(0)
+        load_positions(1)
+        load_weights(0)
+
+        dt_bf16 = consts.tile([P, 1], BF16, name="dt_bf16")
+        nc.scalar.dma_start(out=dt_bf16[:], in_=dt.partition_broadcast(P))
+        dt_f32 = consts.tile([P, 1], F32, name="dt_f32")
+        nc.vector.tensor_copy(out=dt_f32[:], in_=dt_bf16[:])
+
+        identity = consts.tile([P, P], F32, name="identity")
+        make_identity(nc, identity[:])
+
+        bias_row = consts.tile([P, N_OUT], BF16, name="bias_row")
+        nc.vector.memset(bias_row[:], 0.0)
+        nc.scalar.dma_start(out=bias_row[0:1, 0:GATES], in_=glu_b1.unsqueeze(0))
+        nc.scalar.dma_start(out=bias_row[0:1, GATES:N_OUT], in_=glu_b2.unsqueeze(0))
+        ones = consts.tile([P, P], BF16, name="ones")
+        nc.vector.memset(ones[:], 1.0)
+
+        table_warmer = consts.tile([P, 1], F32, name="table_warmer")
+        nc.scalar.activation(out=table_warmer[:], in_=dt_f32[:], func=ACT.Sigmoid)
+
+        acc = [sums.tile([P, N_OUT], F32, name="acc%d" % a) for a in range(ROW_TILES)]
+
+        y_next, y_grouped, y_codes, y_scales = {}, {}, {}, {}
+        w_grouped, w_codes, w_scales = {}, {}, {}
+
+        def update_positions(c, h):
+            cols = slice(h * HALF, (h + 1) * HALF)
+            y_next[c, h] = stage.tile([P, ROW_TILES, HALF], BF16, name="y_next")
+            nc.vector.scalar_tensor_tensor(
+                out=y_next[c, h][:],
+                in0=z_rows[c][:, :, cols],
+                scalar=dt_f32[:, 0:1],
+                in1=y_rows[c][:, :, cols],
+                op0=ALU.mult,
+                op1=ALU.add,
+            )
+
+        def transpose_pass(rows, first_mode, grouped_words):
+            bank = banks.tile([P, ROW_TILES, PAIR_HALVES, P], F32, name="bank", tag="bank")
+            first_word = first_mode // 2
+            for a in range(ROW_TILES):
+                words = rows[:, a, :].bitcast(F32)
+                for u in range(PAIR_HALVES):
+                    nc.tensor.transpose(
+                        bank[:, a, u, :],
+                        words[:, first_word + u : first_word + PAIR_HALVES * P : PAIR_HALVES],
+                        identity[:],
+                    )
+            nc.scalar.copy(out=grouped_words, in_=bank[:].rearrange("p a u r -> p a r u"))
+
+        def position_banks(c, h):
+            if h == 0:
+                y_grouped[c] = stage.tile(
+                    [P, CHUNK_PASSES * BATCH * PACK], BF16, name="y_grouped", bufs=2, align_bytes=64
+                )
+            words = y_grouped[c][:].bitcast(F32).rearrange(
+                "p (s a r u) -> p s a r u", s=CHUNK_PASSES, a=ROW_TILES, r=P
+            )
+            return [
+                (y_next[c, h], s * K_PASS, words[:, h * HALF_PASSES + s])
+                for s in range(HALF_PASSES)
+            ]
+
+        def weight_banks(rows, which, c):
+            todo = []
+            for h in range(2):
+                if which == 0:
+                    w_grouped[c, h] = stage.tile(
+                        [P, HALF_PASSES * N_OUT * PACK], BF16, name="w_grouped", align_bytes=64
+                    )
+                words = w_grouped[c, h][:].bitcast(F32).rearrange(
+                    "p (s w a r u) -> p s w a r u", s=HALF_PASSES, w=2, a=ROW_TILES, r=P
+                )
+                for s in range(HALF_PASSES):
+                    todo.append((rows, (h * HALF_PASSES + s) * K_PASS, words[:, s, which]))
+            return todo
+
+        def quantise(grouped, columns, name):
+            codes = stage.tile([P, columns], U32, name=name + "_codes", align_bytes=64)
+            scales = stage.tile([P, columns], U8, name=name + "_scales", align_bytes=64)
+            nc.vector.quantize_mx(out=codes[:].bitcast(FP8X4), scales=scales[:], in_=grouped[:])
+            return codes, scales
+
+        def quantise_positions(c):
+            y_codes[c], y_scales[c] = quantise(y_grouped[c], CHUNK_PASSES * BATCH, "y")
+
+        def quantise_weights(c, h):
+            w_codes[c, h], w_scales[c, h] = quantise(w_grouped[c, h], HALF_PASSES * N_OUT, "w")
+
+        def multiply_pass(c, s):
+            g = c * CHUNK_PASSES + s
+            h, s_in_half = divmod(s, HALF_PASSES)
+            n_cols = slice(s_in_half * N_OUT, (s_in_half + 1) * N_OUT)
+            for a in range(ROW_TILES):
+                m_cols = slice((s * ROW_TILES + a) * P, (s * ROW_TILES + a + 1) * P)
+                nc.tensor.matmul_mx(
+                    out=acc[a][:],
+                    lhsT=y_codes[c][:, m_cols].bitcast(FP8X4),
+                    lhsT_scale=y_scales[c][:, m_cols],
+                    rhs=w_codes[c, h][:, n_cols].bitcast(FP8X4),
+                    rhs_scale=w_scales[c, h][:, n_cols],
+                    start=(g == 0),
+                    stop=(g == PASSES - 1),
+                )
+
+        for h in range(2):
+            update_positions(0, h)
+            for bank_args in position_banks(0, h):
+                transpose_pass(*bank_args)
+        for c in range(CHUNKS):
+            more = c + 1 < CHUNKS
+            if c + 2 < CHUNKS:
+                load_positions(c + 2)
+            if more:
+                load_weights(c + 1)
+                update_positions(c + 1, 0)
+            if c > 0:
+                quantise_weights(c - 1, 0)
+                quantise_weights(c - 1, 1)
+            if more:
+                update_positions(c + 1, 1)
+            quantise_positions(c)
+
+            todo = weight_banks(w1_rows[c], 0, c)
+            if more:
+                todo.extend(position_banks(c + 1, 0))
+            todo.extend(weight_banks(w2_rows[c], 1, c))
+            if more:
+                todo.extend(position_banks(c + 1, 1))
+            passes_done = 0
+            for i, bank_args in enumerate(todo):
+                transpose_pass(*bank_args)
+                if c > 0 and (i + 1) % BANKS_PER_PASS == 0:
+                    multiply_pass(c - 1, passes_done)
+                    passes_done += 1
+            if c > 0:
+                for s in range(passes_done, CHUNK_PASSES):
+                    multiply_pass(c - 1, s)
+
+        bias_bank = banks.tile([P, N_OUT], F32, name="bias_bank", tag="bank")
+        nc.tensor.matmul(out=bias_bank[:], lhsT=ones[:], rhs=bias_row[:], start=True, stop=True)
+        bias = consts.tile([P, N_OUT], F32, name="bias")
+        nc.scalar.copy(out=bias[:], in_=bias_bank[:])
+
+        quantise_weights(CHUNKS - 1, 0)
+        quantise_weights(CHUNKS - 1, 1)
+        for s in range(CHUNK_PASSES):
+            multiply_pass(CHUNKS - 1, s)
+
+        biased, gate = [], []
+        for a in range(ROW_TILES):
+            biased.append(finish.tile([P, N_OUT], F32, name="biased"))
+            nc.vector.tensor_tensor(out=biased[a][:], in0=acc[a][:], in1=bias[:], op=ALU.add)
+        for a in range(ROW_TILES):
+            gate.append(finish.tile([P, GATES], F32, name="gate"))
+            nc.scalar.activation(out=gate[a][:], in_=biased[a][:, 0:GATES], func=ACT.Sigmoid)
+        for a in range(ROW_TILES):
+            result = finish.tile([P, GATES], F32, name="result")
+            nc.vector.tensor_mul(out=result[:], in0=gate[a][:], in1=biased[a][:, GATES:N_OUT])
+            nc.sync.dma_start(out=out[a * P : (a + 1) * P, :], in_=result[:])

@@ -12,24 +12,17 @@ ALU = mybir.AluOpType
 ACT = mybir.ActivationFunctionType
 
 BATCH, MODES, GATES = 256, 16384, 256
-
 P = 128
 PACK = 4
 K_PASS = P * PACK
 PASSES = MODES // K_PASS
 ROW_TILES = 2
 PAIR_HALVES = 2
-
-CHUNK_PASSES = 4
-CHUNK = CHUNK_PASSES * K_PASS
-CHUNKS = PASSES // CHUNK_PASSES
-HALF_PASSES = CHUNK_PASSES // 2
-HALF = HALF_PASSES * K_PASS
-
-BANKS_PER_PASS = 3
-
+CHUNK_PASSES = (2, 4, 4, 4, 4, 4, 4, 2, 2, 2)
+CHUNKS = len(CHUNK_PASSES)
+FIRST_PASS = tuple(sum(CHUNK_PASSES[:c]) for c in range(CHUNKS))
 N_OUT = 2 * GATES
-
+RUN_BANKS = 6
 FLOPS = 2 * BATCH * MODES * N_OUT
 
 
@@ -39,30 +32,36 @@ def tile_instrumentedlocmblock_pb_k_kernel(
     nc = tc.nc
     with ExitStack() as ctx:
         consts = ctx.enter_context(tc.tile_pool(name="consts", bufs=1))
-        loads = ctx.enter_context(tc.tile_pool(name="loads", bufs=3))
+        loads = ctx.enter_context(tc.tile_pool(name="loads", bufs=4))
         stage = ctx.enter_context(tc.tile_pool(name="stage", bufs=3))
         finish = ctx.enter_context(tc.tile_pool(name="finish", bufs=2))
         banks = ctx.enter_context(tc.psum_pool(name="banks", bufs=6))
         sums = ctx.enter_context(tc.psum_pool(name="sums", bufs=1))
         ctx.enter_context(tc.manual_schedule())
 
-        def load(src, c, name):
-            rows = loads.tile([P, ROW_TILES, CHUNK], BF16, name=name)
-            nc.sync.dma_start(
-                out=rows[:],
-                in_=src.rearrange("(a p) k -> p a k", p=P)[:, :, c * CHUNK : (c + 1) * CHUNK],
-            )
+        def load(src, c, name, bufs):
+            width = CHUNK_PASSES[c] * K_PASS
+            rows = loads.tile([P, ROW_TILES, width], BF16, name=name, bufs=bufs)
+            cols = slice(FIRST_PASS[c] * K_PASS, FIRST_PASS[c] * K_PASS + width)
+            view = src.rearrange("(a p) k -> p a k", p=P)
+            if CHUNK_PASSES[c] > 4:
+                for a in range(ROW_TILES):
+                    nc.sync.dma_start(out=rows[:, a, :], in_=view[:, a, cols])
+            else:
+                nc.sync.dma_start(out=rows[:], in_=view[:, :, cols])
             return rows
 
         y_rows, z_rows, w1_rows, w2_rows = {}, {}, {}, {}
 
         def load_positions(c):
-            y_rows[c] = load(y_tilde, c, "y_rows")
-            z_rows[c] = load(z_next, c, "z_rows")
+            if c < CHUNKS:
+                y_rows[c] = load(y_tilde, c, "y_rows", 3)
+                z_rows[c] = load(z_next, c, "z_rows", 3)
 
         def load_weights(c):
-            w1_rows[c] = load(glu_w1, c, "w1_rows")
-            w2_rows[c] = load(glu_w2, c, "w2_rows")
+            if c < CHUNKS:
+                w1_rows[c] = load(glu_w1, c, "w1_rows", 3)
+                w2_rows[c] = load(glu_w2, c, "w2_rows", 3)
 
         load_positions(0)
         load_positions(1)
@@ -72,148 +71,147 @@ def tile_instrumentedlocmblock_pb_k_kernel(
         nc.scalar.dma_start(out=dt_bf16[:], in_=dt.partition_broadcast(P))
         dt_f32 = consts.tile([P, 1], F32, name="dt_f32")
         nc.vector.tensor_copy(out=dt_f32[:], in_=dt_bf16[:])
-
         identity = consts.tile([P, P], F32, name="identity")
         make_identity(nc, identity[:])
-
         bias_row = consts.tile([P, N_OUT], BF16, name="bias_row")
         nc.vector.memset(bias_row[:], 0.0)
         nc.scalar.dma_start(out=bias_row[0:1, 0:GATES], in_=glu_b1.unsqueeze(0))
         nc.scalar.dma_start(out=bias_row[0:1, GATES:N_OUT], in_=glu_b2.unsqueeze(0))
         ones = consts.tile([P, P], BF16, name="ones")
         nc.vector.memset(ones[:], 1.0)
-
         table_warmer = consts.tile([P, 1], F32, name="table_warmer")
         nc.scalar.activation(out=table_warmer[:], in_=dt_f32[:], func=ACT.Sigmoid)
-
         acc = [sums.tile([P, N_OUT], F32, name="acc%d" % a) for a in range(ROW_TILES)]
 
         y_next, y_grouped, y_codes, y_scales = {}, {}, {}, {}
         w_grouped, w_codes, w_scales = {}, {}, {}
 
-        def update_positions(c, h):
-            cols = slice(h * HALF, (h + 1) * HALF)
-            y_next[c, h] = stage.tile([P, ROW_TILES, HALF], BF16, name="y_next")
-            nc.vector.scalar_tensor_tensor(
-                out=y_next[c, h][:],
-                in0=z_rows[c][:, :, cols],
-                scalar=dt_f32[:, 0:1],
-                in1=y_rows[c][:, :, cols],
-                op0=ALU.mult,
-                op1=ALU.add,
-            )
+        def update_positions(c):
+            if c >= CHUNKS:
+                return
+            width = CHUNK_PASSES[c] * K_PASS
+            half = ROW_TILES * width // 2
+            y_next[c] = stage.tile([P, PAIR_HALVES, half], BF16, name="y_next", bufs=2)
+            zv = z_rows[c][:].rearrange("p a (m u e) -> p u (a m) e", u=2, e=2)
+            yv = y_rows[c][:].rearrange("p a (m u e) -> p u (a m) e", u=2, e=2)
+            for u in range(PAIR_HALVES):
+                nc.vector.scalar_tensor_tensor(
+                    out=y_next[c][:, u, :].rearrange("p (m e) -> p m e", e=2),
+                    in0=zv[:, u],
+                    scalar=dt_f32[:, 0:1],
+                    in1=yv[:, u],
+                    op0=ALU.mult,
+                    op1=ALU.add,
+                )
 
-        def transpose_pass(rows, first_mode, grouped_words):
-            bank = banks.tile([P, ROW_TILES, PAIR_HALVES, P], F32, name="bank", tag="bank")
-            first_word = first_mode // 2
-            for a in range(ROW_TILES):
-                words = rows[:, a, :].bitcast(F32)
-                for u in range(PAIR_HALVES):
-                    nc.tensor.transpose(
-                        bank[:, a, u, :],
-                        words[:, first_word + u : first_word + PAIR_HALVES * P : PAIR_HALVES],
-                        identity[:],
-                    )
-            nc.scalar.copy(out=grouped_words, in_=bank[:].rearrange("p a u r -> p a r u"))
+        copies = [0]
 
-        def position_banks(c, h):
-            if h == 0:
+        def copy_out(bank, grouped_words, share):
+            src = bank[:].rearrange("p a u r -> p a r u")
+            copies[0] += 1
+            if share and copies[0] % 2:
+                nc.vector.tensor_copy(out=grouped_words, in_=src)
+            else:
+                nc.scalar.copy(out=grouped_words, in_=src)
+
+        def position_bank(c, s):
+            if s == 0:
                 y_grouped[c] = stage.tile(
-                    [P, CHUNK_PASSES * BATCH * PACK], BF16, name="y_grouped", bufs=2, align_bytes=64
+                    [P, CHUNK_PASSES[c] * BATCH * PACK], BF16, name="y_grouped", bufs=2, align_bytes=64
                 )
-            words = y_grouped[c][:].bitcast(F32).rearrange(
-                "p (s a r u) -> p s a r u", s=CHUNK_PASSES, a=ROW_TILES, r=P
-            )
-            return [
-                (y_next[c, h], s * K_PASS, words[:, h * HALF_PASSES + s])
-                for s in range(HALF_PASSES)
-            ]
+            out_words = y_grouped[c][:].bitcast(F32).rearrange(
+                "p (s a r u) -> p s a r u", s=CHUNK_PASSES[c], a=ROW_TILES, r=P
+            )[:, s]
+            bank = banks.tile([P, ROW_TILES, PAIR_HALVES, P], F32, name="bank", tag="bank")
+            words = y_next[c][:].bitcast(F32).rearrange("p u (a s i) -> p u a s i", a=ROW_TILES, i=P)
+            for a in range(ROW_TILES):
+                for u in range(PAIR_HALVES):
+                    nc.tensor.transpose(bank[:, a, u, :], words[:, u, a, s, :], identity[:])
+            copy_out(bank, out_words, False)
 
-        def weight_banks(rows, which, c):
-            todo = []
-            for h in range(2):
-                if which == 0:
-                    w_grouped[c, h] = stage.tile(
-                        [P, HALF_PASSES * N_OUT * PACK], BF16, name="w_grouped", align_bytes=64
-                    )
-                words = w_grouped[c, h][:].bitcast(F32).rearrange(
-                    "p (s w a r u) -> p s w a r u", s=HALF_PASSES, w=2, a=ROW_TILES, r=P
-                )
-                for s in range(HALF_PASSES):
-                    todo.append((rows, (h * HALF_PASSES + s) * K_PASS, words[:, s, which]))
-            return todo
+        def groups(c):
+            n = CHUNK_PASSES[c]
+            size = 1 if c >= CHUNKS - 1 else 2
+            return [(s, size) for s in range(0, n, size)]
 
-        def quantise(grouped, columns, name):
-            codes = stage.tile([P, columns], U32, name=name + "_codes", align_bytes=64)
-            scales = stage.tile([P, columns], U8, name=name + "_scales", align_bytes=64)
+        def weight_bank(c, which, s):
+            rows = (w1_rows, w2_rows)[which][c]
+            for first, size in groups(c):
+                if first <= s < first + size:
+                    g = (c, first)
+                    if g not in w_grouped:
+                        w_grouped[g] = stage.tile([P, size * N_OUT * PACK], BF16, name="w_grouped", align_bytes=64, bufs=4)
+                    out_words = w_grouped[g][:].bitcast(F32).rearrange(
+                        "p (s w a r u) -> p s w a r u", s=size, w=2, a=ROW_TILES, r=P
+                    )[:, s - first, which]
+            bank = banks.tile([P, ROW_TILES, PAIR_HALVES, P], F32, name="bank", tag="bank")
+            for a in range(ROW_TILES):
+                words = rows[:, a, :].bitcast(F32)[:, s * 2 * P : (s + 1) * 2 * P]
+                for u in range(PAIR_HALVES):
+                    nc.tensor.transpose(bank[:, a, u, :], words[:, u : 2 * P : 2], identity[:])
+            copy_out(bank, out_words, c >= CHUNKS - 1 and which == 1)
+
+        def quantise(grouped, columns, name, bufs):
+            codes = stage.tile([P, columns], U32, name=name + "_codes", align_bytes=64, bufs=bufs)
+            scales = stage.tile([P, columns], U8, name=name + "_scales", align_bytes=64, bufs=bufs)
             nc.vector.quantize_mx(out=codes[:].bitcast(FP8X4), scales=scales[:], in_=grouped[:])
             return codes, scales
 
         def quantise_positions(c):
-            y_codes[c], y_scales[c] = quantise(y_grouped[c], CHUNK_PASSES * BATCH, "y")
+            y_codes[c], y_scales[c] = quantise(y_grouped[c], CHUNK_PASSES[c] * BATCH, "y", 3)
 
-        def quantise_weights(c, h):
-            w_codes[c, h], w_scales[c, h] = quantise(w_grouped[c, h], HALF_PASSES * N_OUT, "w")
+        def quantise_weights(c):
+            for g in groups(c):
+                w_codes[c, g[0]], w_scales[c, g[0]] = quantise(w_grouped[c, g[0]], g[1] * N_OUT, "w", 4)
 
-        def multiply_pass(c, s):
-            g = c * CHUNK_PASSES + s
-            h, s_in_half = divmod(s, HALF_PASSES)
-            n_cols = slice(s_in_half * N_OUT, (s_in_half + 1) * N_OUT)
-            for a in range(ROW_TILES):
-                m_cols = slice((s * ROW_TILES + a) * P, (s * ROW_TILES + a + 1) * P)
-                nc.tensor.matmul_mx(
-                    out=acc[a][:],
-                    lhsT=y_codes[c][:, m_cols].bitcast(FP8X4),
-                    lhsT_scale=y_scales[c][:, m_cols],
-                    rhs=w_codes[c, h][:, n_cols].bitcast(FP8X4),
-                    rhs_scale=w_scales[c, h][:, n_cols],
-                    start=(g == 0),
-                    stop=(g == PASSES - 1),
-                )
+        def multiply(c, s, a):
+            g = FIRST_PASS[c] + s
+            for first, size in groups(c):
+                if first <= s < first + size:
+                    n_cols = slice((s - first) * N_OUT, (s - first + 1) * N_OUT)
+                    m_cols = slice((s * ROW_TILES + a) * P, (s * ROW_TILES + a + 1) * P)
+                    nc.tensor.matmul_mx(
+                        out=acc[a][:],
+                        lhsT=y_codes[c][:, m_cols].bitcast(FP8X4),
+                        lhsT_scale=y_scales[c][:, m_cols],
+                        rhs=w_codes[c, first][:, n_cols].bitcast(FP8X4),
+                        rhs_scale=w_scales[c, first][:, n_cols],
+                        start=(g == 0),
+                        stop=(g == PASSES - 1),
+                    )
 
-        for h in range(2):
-            update_positions(0, h)
-            for bank_args in position_banks(0, h):
-                transpose_pass(*bank_args)
+        update_positions(0)
+        for s in range(CHUNK_PASSES[0]):
+            position_bank(0, s)
         for c in range(CHUNKS):
-            more = c + 1 < CHUNKS
-            if c + 2 < CHUNKS:
-                load_positions(c + 2)
-            if more:
-                load_weights(c + 1)
-                update_positions(c + 1, 0)
+            load_positions(c + 2)
+            load_weights(c + 1)
             if c > 0:
-                quantise_weights(c - 1, 0)
-                quantise_weights(c - 1, 1)
-            if more:
-                update_positions(c + 1, 1)
+                quantise_weights(c - 1)
+            update_positions(c + 1)
             quantise_positions(c)
-
-            todo = weight_banks(w1_rows[c], 0, c)
-            if more:
-                todo.extend(position_banks(c + 1, 0))
-            todo.extend(weight_banks(w2_rows[c], 1, c))
-            if more:
-                todo.extend(position_banks(c + 1, 1))
-            passes_done = 0
-            for i, bank_args in enumerate(todo):
-                transpose_pass(*bank_args)
-                if c > 0 and (i + 1) % BANKS_PER_PASS == 0:
-                    multiply_pass(c - 1, passes_done)
-                    passes_done += 1
-            if c > 0:
-                for s in range(passes_done, CHUNK_PASSES):
-                    multiply_pass(c - 1, s)
+            todo = [(weight_bank, (c, which, s)) for which in range(2) for s in range(CHUNK_PASSES[c])]
+            if c + 1 < CHUNKS:
+                todo += [(position_bank, (c + 1, s)) for s in range(CHUNK_PASSES[c + 1])]
+            mms = [(s, a) for s in range(CHUNK_PASSES[c - 1]) for a in range(ROW_TILES)] if c > 0 else []
+            runs = [todo[i : i + RUN_BANKS] for i in range(0, len(todo), RUN_BANKS)]
+            per = -(-len(mms) // len(runs)) if mms else 0
+            for r in runs:
+                for f, args in r:
+                    f(*args)
+                for s, a in mms[:per]:
+                    multiply(c - 1, s, a)
+                mms = mms[per:]
 
         bias_bank = banks.tile([P, N_OUT], F32, name="bias_bank", tag="bank")
         nc.tensor.matmul(out=bias_bank[:], lhsT=ones[:], rhs=bias_row[:], start=True, stop=True)
         bias = consts.tile([P, N_OUT], F32, name="bias")
         nc.scalar.copy(out=bias[:], in_=bias_bank[:])
 
-        quantise_weights(CHUNKS - 1, 0)
-        quantise_weights(CHUNKS - 1, 1)
-        for s in range(CHUNK_PASSES):
-            multiply_pass(CHUNKS - 1, s)
+        quantise_weights(CHUNKS - 1)
+        for a in range(ROW_TILES):
+            for s in range(CHUNK_PASSES[CHUNKS - 1]):
+                multiply(CHUNKS - 1, s, a)
 
         biased, gate = [], []
         for a in range(ROW_TILES):

@@ -22,7 +22,7 @@ CHUNK_PASSES = (2, 4, 4, 4, 4, 4, 4, 2, 2, 2)
 CHUNKS = len(CHUNK_PASSES)
 FIRST_PASS = tuple(sum(CHUNK_PASSES[:c]) for c in range(CHUNKS))
 N_OUT = 2 * GATES
-RUN_BANKS = 6
+RUN_BANKS = 3
 FLOPS = 2 * BATCH * MODES * N_OUT
 
 

@@ -18,12 +18,11 @@ K_PASS = P * PACK
 PASSES = MODES // K_PASS
 ROW_TILES = 2
 PAIR_HALVES = 2
-CHUNK_PASSES = (2, 4, 4, 4, 4, 4, 4, 2, 2, 2)
+CHUNK_PASSES = (4, 4, 4, 4, 4, 4, 4, 4)
 CHUNKS = len(CHUNK_PASSES)
 FIRST_PASS = tuple(sum(CHUNK_PASSES[:c]) for c in range(CHUNKS))
-N_OUT = 2 * GATES
-RUN_BANKS = 3
-FLOPS = 2 * BATCH * MODES * N_OUT
+LAST_W2 = (2, 1, 1,)
+FLOPS = 2 * BATCH * MODES * 2 * GATES
 
 
 def tile_instrumentedlocmblock_pb_k_kernel(
@@ -32,124 +31,124 @@ def tile_instrumentedlocmblock_pb_k_kernel(
     nc = tc.nc
     with ExitStack() as ctx:
         consts = ctx.enter_context(tc.tile_pool(name="consts", bufs=1))
-        loads = ctx.enter_context(tc.tile_pool(name="loads", bufs=4))
+        loads = ctx.enter_context(tc.tile_pool(name="loads", bufs=3))
         stage = ctx.enter_context(tc.tile_pool(name="stage", bufs=3))
         finish = ctx.enter_context(tc.tile_pool(name="finish", bufs=2))
-        banks = ctx.enter_context(tc.psum_pool(name="banks", bufs=6))
+        banks = ctx.enter_context(tc.psum_pool(name="banks", bufs=4))
         sums = ctx.enter_context(tc.psum_pool(name="sums", bufs=1))
         ctx.enter_context(tc.manual_schedule())
 
-        def load(src, c, name, bufs):
-            width = CHUNK_PASSES[c] * K_PASS
-            rows = loads.tile([P, ROW_TILES, width], BF16, name=name, bufs=bufs)
-            cols = slice(FIRST_PASS[c] * K_PASS, FIRST_PASS[c] * K_PASS + width)
-            view = src.rearrange("(a p) k -> p a k", p=P)
-            if CHUNK_PASSES[c] > 4:
-                for a in range(ROW_TILES):
-                    nc.sync.dma_start(out=rows[:, a, :], in_=view[:, a, cols])
-            else:
-                nc.sync.dma_start(out=rows[:], in_=view[:, :, cols])
-            return rows
-
-        y_rows, z_rows, w1_rows, w2_rows = {}, {}, {}, {}
-
-        def load_positions(c):
-            if c < CHUNKS:
-                y_rows[c] = load(y_tilde, c, "y_rows", 3)
-                z_rows[c] = load(z_next, c, "z_rows", 3)
-
-        def load_weights(c):
-            if c < CHUNKS:
-                w1_rows[c] = load(glu_w1, c, "w1_rows", 3)
-                w2_rows[c] = load(glu_w2, c, "w2_rows", 3)
-
-        load_positions(0)
-        load_positions(1)
-        load_weights(0)
-
         dt_bf16 = consts.tile([P, 1], BF16, name="dt_bf16")
         nc.scalar.dma_start(out=dt_bf16[:], in_=dt.partition_broadcast(P))
+        bias_row = consts.tile([P, 2 * GATES], BF16, name="bias_row")
+        nc.vector.memset(bias_row[:], 0.0)
+        nc.scalar.dma_start(out=bias_row[0:1, 0:GATES], in_=glu_b1.unsqueeze(0))
+        nc.scalar.dma_start(out=bias_row[0:1, GATES:], in_=glu_b2.unsqueeze(0))
+
+        def load(src, first, n, name, bufs):
+            rows = loads.tile([P, ROW_TILES, n * K_PASS], BF16, name=name, bufs=bufs)
+            view = src.rearrange("(a p) k -> p a k", p=P)
+            nc.sync.dma_start(out=rows[:], in_=view[:, :, first * K_PASS : (first + n) * K_PASS])
+            return rows
+
+        y_rows, z_rows, w_rows = {}, {}, {}
+
+        def load_positions(c, a):
+            if c < CHUNKS:
+                n = CHUNK_PASSES[c]
+                cols = slice(FIRST_PASS[c] * K_PASS, (FIRST_PASS[c] + n) * K_PASS)
+                for src, name, keep in ((y_tilde, "y_rows", y_rows), (z_next, "z_rows", z_rows)):
+                    keep[c, a] = loads.tile([P, n * K_PASS], BF16, name=name, bufs=8)
+                    nc.sync.dma_start(out=keep[c, a][:], in_=src[a * P : (a + 1) * P, cols])
+
+        def load_step(c):
+            load_weights(c, 0)
+            load_positions(c + 1, 0)
+            load_weights(c, 1)
+            load_positions(c + 1, 1)
+
+        def pieces(c, which):
+            sizes = LAST_W2 if which == 1 and c == CHUNKS - 1 else (CHUNK_PASSES[c],)
+            return [(which, FIRST_PASS[c] + sum(sizes[:i]), n) for i, n in enumerate(sizes)]
+
+        def load_weights(c, which):
+            if c < CHUNKS:
+                for piece in pieces(c, which):
+                    w_rows[piece] = load((glu_w1, glu_w2)[which], piece[1], piece[2], "w_rows", 8)
+
+        load_positions(0, 0)
+        load_positions(0, 1)
+        for c in range(3):
+            load_step(c)
+
         dt_f32 = consts.tile([P, 1], F32, name="dt_f32")
         nc.vector.tensor_copy(out=dt_f32[:], in_=dt_bf16[:])
         identity = consts.tile([P, P], F32, name="identity")
         make_identity(nc, identity[:])
-        bias_row = consts.tile([P, N_OUT], BF16, name="bias_row")
-        nc.vector.memset(bias_row[:], 0.0)
-        nc.scalar.dma_start(out=bias_row[0:1, 0:GATES], in_=glu_b1.unsqueeze(0))
-        nc.scalar.dma_start(out=bias_row[0:1, GATES:N_OUT], in_=glu_b2.unsqueeze(0))
         ones = consts.tile([P, P], BF16, name="ones")
         nc.vector.memset(ones[:], 1.0)
         table_warmer = consts.tile([P, 1], F32, name="table_warmer")
         nc.scalar.activation(out=table_warmer[:], in_=dt_f32[:], func=ACT.Sigmoid)
-        acc = [sums.tile([P, N_OUT], F32, name="acc%d" % a) for a in range(ROW_TILES)]
+        acc = {}
+        for which in range(2):
+            for a in range(ROW_TILES):
+                acc[which, a] = sums.tile([P, GATES], F32, name="acc%d%d" % (which, a))
 
-        y_next, y_grouped, y_codes, y_scales = {}, {}, {}, {}
-        w_grouped, w_codes, w_scales = {}, {}, {}
+        y_next, y_grouped, y_codes, w_grouped, w_codes = {}, {}, {}, {}, {}
 
-        def update_positions(c):
+        def update_positions(c, a):
             if c >= CHUNKS:
                 return
-            width = CHUNK_PASSES[c] * K_PASS
-            half = ROW_TILES * width // 2
-            y_next[c] = stage.tile([P, PAIR_HALVES, half], BF16, name="y_next", bufs=2)
-            zv = z_rows[c][:].rearrange("p a (m u e) -> p u (a m) e", u=2, e=2)
-            yv = y_rows[c][:].rearrange("p a (m u e) -> p u (a m) e", u=2, e=2)
-            for u in range(PAIR_HALVES):
+            half = CHUNK_PASSES[c] * K_PASS // 2
+            y_next[c, a] = stage.tile([P, 2, half], BF16, name="y_next", bufs=4)
+            split = "p (m u e) -> p u m e"
+            for u in range(2):
                 nc.vector.scalar_tensor_tensor(
-                    out=y_next[c][:, u, :].rearrange("p (m e) -> p m e", e=2),
-                    in0=zv[:, u],
+                    out=y_next[c, a][:, u, :].rearrange("p (m e) -> p m e", e=2),
+                    in0=z_rows[c, a][:].rearrange(split, u=2, e=2)[:, u],
                     scalar=dt_f32[:, 0:1],
-                    in1=yv[:, u],
+                    in1=y_rows[c, a][:].rearrange(split, u=2, e=2)[:, u],
                     op0=ALU.mult,
                     op1=ALU.add,
                 )
 
-        copies = [0]
+        def new_bank():
+            return banks.tile([P, ROW_TILES, PAIR_HALVES, P], F32, name="bank", tag="bank")
 
-        def copy_out(bank, grouped_words, share):
+        def copy_out(bank, grouped, s, n, on_vector):
+            words = grouped[:].bitcast(F32).rearrange("p (s a r u) -> p s a r u", s=n, a=ROW_TILES, r=P)[:, s]
             src = bank[:].rearrange("p a u r -> p a r u")
-            copies[0] += 1
-            if share and copies[0] % 2:
-                nc.vector.tensor_copy(out=grouped_words, in_=src)
+            if on_vector:
+                nc.vector.tensor_copy(out=words, in_=src)
             else:
-                nc.scalar.copy(out=grouped_words, in_=src)
+                nc.scalar.copy(out=words, in_=src)
 
-        def position_bank(c, s):
-            if s == 0:
-                y_grouped[c] = stage.tile(
-                    [P, CHUNK_PASSES[c] * BATCH * PACK], BF16, name="y_grouped", bufs=2, align_bytes=64
-                )
-            out_words = y_grouped[c][:].bitcast(F32).rearrange(
-                "p (s a r u) -> p s a r u", s=CHUNK_PASSES[c], a=ROW_TILES, r=P
-            )[:, s]
-            bank = banks.tile([P, ROW_TILES, PAIR_HALVES, P], F32, name="bank", tag="bank")
-            words = y_next[c][:].bitcast(F32).rearrange("p u (a s i) -> p u a s i", a=ROW_TILES, i=P)
-            for a in range(ROW_TILES):
-                for u in range(PAIR_HALVES):
-                    nc.tensor.transpose(bank[:, a, u, :], words[:, u, a, s, :], identity[:])
-            copy_out(bank, out_words, False)
-
-        def groups(c):
+        def transpose_positions(c, a):
+            if c >= CHUNKS:
+                return
             n = CHUNK_PASSES[c]
-            size = 1 if c >= CHUNKS - 1 else 2
-            return [(s, size) for s in range(0, n, size)]
+            if a == 0:
+                y_grouped[c] = stage.tile([P, n * BATCH * PACK], BF16, name="y_grouped", bufs=2, align_bytes=64)
+            words = y_next[c, a][:].bitcast(F32).rearrange("p u (s i) -> p u s i", i=P)
+            out_words = y_grouped[c][:].bitcast(F32).rearrange("p (s a r u) -> p s a r u", s=n, a=ROW_TILES, r=P)[:, :, a]
+            for s0 in range(0, n, 2):
+                bank = banks.tile([P, 2, 2, P], F32, name="bank", tag="bank")
+                for s in range(2):
+                    for u in range(2):
+                        nc.tensor.transpose(bank[:, s, u, :], words[:, u, s0 + s, :], identity[:])
+                nc.scalar.copy(out=out_words[:, s0 : s0 + 2], in_=bank[:].rearrange("p s u r -> p s r u"))
 
-        def weight_bank(c, which, s):
-            rows = (w1_rows, w2_rows)[which][c]
-            for first, size in groups(c):
-                if first <= s < first + size:
-                    g = (c, first)
-                    if g not in w_grouped:
-                        w_grouped[g] = stage.tile([P, size * N_OUT * PACK], BF16, name="w_grouped", align_bytes=64, bufs=4)
-                    out_words = w_grouped[g][:].bitcast(F32).rearrange(
-                        "p (s w a r u) -> p s w a r u", s=size, w=2, a=ROW_TILES, r=P
-                    )[:, s - first, which]
-            bank = banks.tile([P, ROW_TILES, PAIR_HALVES, P], F32, name="bank", tag="bank")
-            for a in range(ROW_TILES):
-                words = rows[:, a, :].bitcast(F32)[:, s * 2 * P : (s + 1) * 2 * P]
-                for u in range(PAIR_HALVES):
-                    nc.tensor.transpose(bank[:, a, u, :], words[:, u : 2 * P : 2], identity[:])
-            copy_out(bank, out_words, c >= CHUNKS - 1 and which == 1)
+        def transpose_weights(piece, part, vec=()):
+            n = piece[2]
+            if 0 in part:
+                w_grouped[piece] = stage.tile([P, n * GATES * PACK], BF16, name="w_grouped", bufs=3, align_bytes=64)
+            for s in part:
+                bank = new_bank()
+                for a in range(ROW_TILES):
+                    words = w_rows[piece][:, a, :].bitcast(F32)[:, s * 2 * P : (s + 1) * 2 * P]
+                    for u in range(PAIR_HALVES):
+                        nc.tensor.transpose(bank[:, a, u, :], words[:, u : 2 * P : 2], identity[:])
+                copy_out(bank, w_grouped[piece], s, n, s in vec)
 
         def quantise(grouped, columns, name, bufs):
             codes = stage.tile([P, columns], U32, name=name + "_codes", align_bytes=64, bufs=bufs)
@@ -158,69 +157,82 @@ def tile_instrumentedlocmblock_pb_k_kernel(
             return codes, scales
 
         def quantise_positions(c):
-            y_codes[c], y_scales[c] = quantise(y_grouped[c], CHUNK_PASSES[c] * BATCH, "y", 3)
+            if c < CHUNKS:
+                y_codes[c] = quantise(y_grouped[c], CHUNK_PASSES[c] * BATCH, "y", 3)
 
-        def quantise_weights(c):
-            for g in groups(c):
-                w_codes[c, g[0]], w_scales[c, g[0]] = quantise(w_grouped[c, g[0]], g[1] * N_OUT, "w", 4)
+        def quantise_weights(piece):
+            w_codes[piece] = quantise(w_grouped[piece], piece[2] * GATES, "w", 3)
 
-        def multiply(c, s, a):
-            g = FIRST_PASS[c] + s
-            for first, size in groups(c):
-                if first <= s < first + size:
-                    n_cols = slice((s - first) * N_OUT, (s - first + 1) * N_OUT)
-                    m_cols = slice((s * ROW_TILES + a) * P, (s * ROW_TILES + a + 1) * P)
+        def multiply(c, piece):
+            which, first, n = piece
+            for a in range(ROW_TILES):
+                for s in range(n):
+                    g = first + s
+                    n_cols = slice(s * GATES, (s + 1) * GATES)
+                    m0 = ((g - FIRST_PASS[c]) * ROW_TILES + a) * P
+                    m_cols = slice(m0, m0 + P)
                     nc.tensor.matmul_mx(
-                        out=acc[a][:],
-                        lhsT=y_codes[c][:, m_cols].bitcast(FP8X4),
-                        lhsT_scale=y_scales[c][:, m_cols],
-                        rhs=w_codes[c, first][:, n_cols].bitcast(FP8X4),
-                        rhs_scale=w_scales[c, first][:, n_cols],
+                        out=acc[which, a][:],
+                        lhsT=y_codes[c][0][:, m_cols].bitcast(FP8X4),
+                        lhsT_scale=y_codes[c][1][:, m_cols],
+                        rhs=w_codes[piece][0][:, n_cols].bitcast(FP8X4),
+                        rhs_scale=w_codes[piece][1][:, n_cols],
                         start=(g == 0),
                         stop=(g == PASSES - 1),
                     )
 
-        update_positions(0)
-        for s in range(CHUNK_PASSES[0]):
-            position_bank(0, s)
+        LAST = CHUNKS - 1
+        biased, gate = {}, {}
+
+        def add_bias(which, a):
+            biased[which, a] = finish.tile([P, GATES], F32, name="biased%d" % which)
+            nc.vector.tensor_tensor(
+                out=biased[which, a][:], in0=acc[which, a][:], in1=bias[:, which * GATES : (which + 1) * GATES], op=ALU.add
+            )
+
+        update_positions(0, 0)
+        transpose_positions(0, 0)
+        update_positions(0, 1)
         for c in range(CHUNKS):
-            load_positions(c + 2)
-            load_weights(c + 1)
+            n = CHUNK_PASSES[c]
+            first_w, second_w = pieces(c, 0)[0], pieces(c, 1)
+            load_step(c + 3)
+            transpose_weights(first_w, range(0, n // 2))
+            transpose_positions(c, 1)
+            transpose_weights(first_w, range(n // 2, n))
             if c > 0:
-                quantise_weights(c - 1)
-            update_positions(c + 1)
+                multiply(c - 1, pieces(c - 1, 1)[0])
+            update_positions(c + 1, 0)
             quantise_positions(c)
-            todo = [(weight_bank, (c, which, s)) for which in range(2) for s in range(CHUNK_PASSES[c])]
-            if c + 1 < CHUNKS:
-                todo += [(position_bank, (c + 1, s)) for s in range(CHUNK_PASSES[c + 1])]
-            mms = [(s, a) for s in range(CHUNK_PASSES[c - 1]) for a in range(ROW_TILES)] if c > 0 else []
-            runs = [todo[i : i + RUN_BANKS] for i in range(0, len(todo), RUN_BANKS)]
-            per = -(-len(mms) // len(runs)) if mms else 0
-            for r in runs:
-                for f, args in r:
-                    f(*args)
-                for s, a in mms[:per]:
-                    multiply(c - 1, s, a)
-                mms = mms[per:]
+            quantise_weights(first_w)
+            if c < LAST:
+                transpose_weights(second_w[0], range(0, n // 2))
+                transpose_positions(c + 1, 0)
+                transpose_weights(second_w[0], range(n // 2, n))
+                multiply(c, first_w)
+                update_positions(c + 1, 1)
+                quantise_weights(second_w[0])
+            else:
+                for piece in second_w:
+                    transpose_weights(piece, range(piece[2]), (1,))
+                    pass
+                multiply(c, first_w)
+                for piece in second_w:
+                    quantise_weights(piece)
+                for a in range(ROW_TILES):
+                    add_bias(0, a)
+                    gate[a] = finish.tile([P, GATES], F32, name="gate")
+                    nc.scalar.activation(out=gate[a][:], in_=biased[0, a][:], func=ACT.Sigmoid)
+                for piece in second_w:
+                    multiply(c, piece)
+            if c == LAST - 2:
+                bias_bank = banks.tile([P, 2 * GATES], F32, name="bias_bank", tag="bank")
+                nc.tensor.matmul(out=bias_bank[:], lhsT=ones[:], rhs=bias_row[:], start=True, stop=True)
+                bias = consts.tile([P, 2 * GATES], F32, name="bias")
+                nc.scalar.copy(out=bias[:], in_=bias_bank[:])
 
-        bias_bank = banks.tile([P, N_OUT], F32, name="bias_bank", tag="bank")
-        nc.tensor.matmul(out=bias_bank[:], lhsT=ones[:], rhs=bias_row[:], start=True, stop=True)
-        bias = consts.tile([P, N_OUT], F32, name="bias")
-        nc.scalar.copy(out=bias[:], in_=bias_bank[:])
-
-        quantise_weights(CHUNKS - 1)
         for a in range(ROW_TILES):
-            for s in range(CHUNK_PASSES[CHUNKS - 1]):
-                multiply(CHUNKS - 1, s, a)
-
-        biased, gate = [], []
-        for a in range(ROW_TILES):
-            biased.append(finish.tile([P, N_OUT], F32, name="biased"))
-            nc.vector.tensor_tensor(out=biased[a][:], in0=acc[a][:], in1=bias[:], op=ALU.add)
-        for a in range(ROW_TILES):
-            gate.append(finish.tile([P, GATES], F32, name="gate"))
-            nc.scalar.activation(out=gate[a][:], in_=biased[a][:, 0:GATES], func=ACT.Sigmoid)
-        for a in range(ROW_TILES):
+            add_bias(1, a)
             result = finish.tile([P, GATES], F32, name="result")
-            nc.vector.tensor_mul(out=result[:], in0=gate[a][:], in1=biased[a][:, GATES:N_OUT])
+            nc.vector.tensor_mul(out=result[:], in0=gate[a][:], in1=biased[1, a][:])
             nc.sync.dma_start(out=out[a * P : (a + 1) * P, :], in_=result[:])

@@ -123,15 +123,15 @@ def tile_instrumentedlocmblock_pb_k_kernel(
             else:
                 nc.scalar.copy(out=words, in_=src)
 
-        def transpose_positions(c, a):
+        def transpose_positions(c, a, part):
             if c >= CHUNKS:
                 return
             n = CHUNK_PASSES[c]
-            if a == 0:
+            if a == 0 and 0 in part:
                 y_grouped[c] = stage.tile([P, n * BATCH * PACK], BF16, name="y_grouped", bufs=2, align_bytes=64)
             words = y_next[c, a][:].bitcast(F32).rearrange("p u (s i) -> p u s i", i=P)
             out_words = y_grouped[c][:].bitcast(F32).rearrange("p (s a r u) -> p s a r u", s=n, a=ROW_TILES, r=P)[:, :, a]
-            for s0 in range(0, n, 2):
+            for s0 in part:
                 bank = banks.tile([P, 2, 2, P], F32, name="bank", tag="bank")
                 for s in range(2):
                     for u in range(2):
@@ -163,10 +163,10 @@ def tile_instrumentedlocmblock_pb_k_kernel(
         def quantise_weights(piece):
             w_codes[piece] = quantise(w_grouped[piece], piece[2] * GATES, "w", 3)
 
-        def multiply(c, piece):
+        def multiply(c, piece, part=None):
             which, first, n = piece
             for a in range(ROW_TILES):
-                for s in range(n):
+                for s in range(n) if part is None else part:
                     g = first + s
                     n_cols = slice(s * GATES, (s + 1) * GATES)
                     m0 = ((g - FIRST_PASS[c]) * ROW_TILES + a) * P
@@ -191,25 +191,32 @@ def tile_instrumentedlocmblock_pb_k_kernel(
             )
 
         update_positions(0, 0)
-        transpose_positions(0, 0)
+        transpose_positions(0, 0, range(0, CHUNK_PASSES[0], 2))
         update_positions(0, 1)
         for c in range(CHUNKS):
             n = CHUNK_PASSES[c]
             first_w, second_w = pieces(c, 0)[0], pieces(c, 1)
             load_step(c + 3)
             transpose_weights(first_w, range(0, n // 2))
-            transpose_positions(c, 1)
+            transpose_positions(c, 1, range(0, n // 2, 2))
+            if c > 0:
+                last_w = pieces(c - 1, 1)[0]
+                multiply(c - 1, last_w, range(0, last_w[2] // 2))
+            transpose_positions(c, 1, range(n // 2, n, 2))
             transpose_weights(first_w, range(n // 2, n))
             if c > 0:
-                multiply(c - 1, pieces(c - 1, 1)[0])
+                multiply(c - 1, last_w, range(last_w[2] // 2, last_w[2]))
             update_positions(c + 1, 0)
             quantise_positions(c)
             quantise_weights(first_w)
             if c < LAST:
+                more = CHUNK_PASSES[c + 1]
                 transpose_weights(second_w[0], range(0, n // 2))
-                transpose_positions(c + 1, 0)
+                transpose_positions(c + 1, 0, range(0, more // 2, 2))
+                multiply(c, first_w, range(0, n // 2))
+                transpose_positions(c + 1, 0, range(more // 2, more, 2))
                 transpose_weights(second_w[0], range(n // 2, n))
-                multiply(c, first_w)
+                multiply(c, first_w, range(n // 2, n))
                 update_positions(c + 1, 1)
                 quantise_weights(second_w[0])
             else:

@@ -17,12 +17,17 @@ PACK = 4
 K_PASS = P * PACK
 PASSES = MODES // K_PASS
 ROW_TILES = 2
-PAIR_HALVES = 2
+PAIRS = 2
 CHUNK_PASSES = (4, 4, 4, 4, 4, 4, 4, 4)
 CHUNKS = len(CHUNK_PASSES)
 FIRST_PASS = tuple(sum(CHUNK_PASSES[:c]) for c in range(CHUNKS))
-LAST_W2 = (2, 1, 1,)
+STEPS = 2 * CHUNKS
+LAST_PIECES = (2, 1, 1,)
 FLOPS = 2 * BATCH * MODES * 2 * GATES
+
+
+def halves(n):
+    return range(0, n // 2), range(n // 2, n)
 
 
 def tile_instrumentedlocmblock_pb_k_kernel(
@@ -31,7 +36,7 @@ def tile_instrumentedlocmblock_pb_k_kernel(
     nc = tc.nc
     with ExitStack() as ctx:
         consts = ctx.enter_context(tc.tile_pool(name="consts", bufs=1))
-        loads = ctx.enter_context(tc.tile_pool(name="loads", bufs=3))
+        loads = ctx.enter_context(tc.tile_pool(name="loads", bufs=8))
         stage = ctx.enter_context(tc.tile_pool(name="stage", bufs=3))
         finish = ctx.enter_context(tc.tile_pool(name="finish", bufs=2))
         banks = ctx.enter_context(tc.psum_pool(name="banks", bufs=4))
@@ -45,41 +50,38 @@ def tile_instrumentedlocmblock_pb_k_kernel(
         nc.scalar.dma_start(out=bias_row[0:1, 0:GATES], in_=glu_b1.unsqueeze(0))
         nc.scalar.dma_start(out=bias_row[0:1, GATES:], in_=glu_b2.unsqueeze(0))
 
-        def load(src, first, n, name, bufs):
-            rows = loads.tile([P, ROW_TILES, n * K_PASS], BF16, name=name, bufs=bufs)
-            view = src.rearrange("(a p) k -> p a k", p=P)
-            nc.sync.dma_start(out=rows[:], in_=view[:, :, first * K_PASS : (first + n) * K_PASS])
-            return rows
-
         y_rows, z_rows, w_rows = {}, {}, {}
 
-        def load_positions(c, a):
-            if c < CHUNKS:
-                n = CHUNK_PASSES[c]
-                cols = slice(FIRST_PASS[c] * K_PASS, (FIRST_PASS[c] + n) * K_PASS)
-                for src, name, keep in ((y_tilde, "y_rows", y_rows), (z_next, "z_rows", z_rows)):
-                    keep[c, a] = loads.tile([P, n * K_PASS], BF16, name=name, bufs=8)
-                    nc.sync.dma_start(out=keep[c, a][:], in_=src[a * P : (a + 1) * P, cols])
+        def pieces(h):
+            c, which = divmod(h, 2)
+            sizes = LAST_PIECES if h == STEPS - 1 else (CHUNK_PASSES[c],)
+            return [(h, FIRST_PASS[c] + sum(sizes[:i]), n) for i, n in enumerate(sizes)]
 
-        def load_step(c):
-            load_weights(c, 0)
-            load_positions(c + 1, 0)
-            load_weights(c, 1)
-            load_positions(c + 1, 1)
+        def load_weights(h):
+            src = (glu_w1, glu_w2)[h % 2].rearrange("(a p) k -> p a k", p=P)
+            for piece in pieces(h):
+                first, n = piece[1:]
+                w_rows[piece] = loads.tile([P, ROW_TILES, n * K_PASS], BF16, name="w_rows", bufs=8)
+                nc.sync.dma_start(out=w_rows[piece][:], in_=src[:, :, first * K_PASS : (first + n) * K_PASS])
 
-        def pieces(c, which):
-            sizes = LAST_W2 if which == 1 and c == CHUNKS - 1 else (CHUNK_PASSES[c],)
-            return [(which, FIRST_PASS[c] + sum(sizes[:i]), n) for i, n in enumerate(sizes)]
+        def load_positions(h):
+            if h >= STEPS:
+                return
+            c, a = divmod(h, 2)
+            cols = slice(FIRST_PASS[c] * K_PASS, (FIRST_PASS[c] + CHUNK_PASSES[c]) * K_PASS)
+            for src, name, keep in ((y_tilde, "y_rows", y_rows), (z_next, "z_rows", z_rows)):
+                keep[h] = loads.tile([P, CHUNK_PASSES[c] * K_PASS], BF16, name=name, bufs=8)
+                nc.sync.dma_start(out=keep[h][:], in_=src[a * P : (a + 1) * P, cols])
 
-        def load_weights(c, which):
-            if c < CHUNKS:
-                for piece in pieces(c, which):
-                    w_rows[piece] = load((glu_w1, glu_w2)[which], piece[1], piece[2], "w_rows", 8)
+        def load_step(h):
+            if h < STEPS:
+                load_weights(h)
+                load_positions(h + 2)
 
-        load_positions(0, 0)
-        load_positions(0, 1)
-        for c in range(3):
-            load_step(c)
+        load_positions(0)
+        load_positions(1)
+        for h in range(6):
+            load_step(h)
 
         dt_f32 = consts.tile([P, 1], F32, name="dt_f32")
         nc.vector.tensor_copy(out=dt_f32[:], in_=dt_bf16[:])
@@ -96,148 +98,142 @@ def tile_instrumentedlocmblock_pb_k_kernel(
 
         y_next, y_grouped, y_codes, w_grouped, w_codes = {}, {}, {}, {}, {}
 
-        def update_positions(c, a):
-            if c >= CHUNKS:
+        def update_positions(h):
+            if h >= STEPS:
                 return
-            half = CHUNK_PASSES[c] * K_PASS // 2
-            y_next[c, a] = stage.tile([P, 2, half], BF16, name="y_next", bufs=4)
-            split = "p (m u e) -> p u m e"
-            for u in range(2):
+            y_next[h] = stage.tile([P, PAIRS, CHUNK_PASSES[h // 2] * K_PASS // PAIRS], BF16, name="y_next", bufs=4)
+            for u in range(PAIRS):
                 nc.vector.scalar_tensor_tensor(
-                    out=y_next[c, a][:, u, :].rearrange("p (m e) -> p m e", e=2),
-                    in0=z_rows[c, a][:].rearrange(split, u=2, e=2)[:, u],
+                    out=y_next[h][:, u, :].rearrange("p (m e) -> p m e", e=2),
+                    in0=z_rows[h][:].rearrange("p (m u e) -> p u m e", u=PAIRS, e=2)[:, u],
                     scalar=dt_f32[:, 0:1],
-                    in1=y_rows[c, a][:].rearrange(split, u=2, e=2)[:, u],
+                    in1=y_rows[h][:].rearrange("p (m u e) -> p u m e", u=PAIRS, e=2)[:, u],
                     op0=ALU.mult,
                     op1=ALU.add,
                 )
 
-        def new_bank():
-            return banks.tile([P, ROW_TILES, PAIR_HALVES, P], F32, name="bank", tag="bank")
-
-        def copy_out(bank, grouped, s, n, on_vector):
-            words = grouped[:].bitcast(F32).rearrange("p (s a r u) -> p s a r u", s=n, a=ROW_TILES, r=P)[:, s]
-            src = bank[:].rearrange("p a u r -> p a r u")
+        def copy_out(bank, words, on_vector):
+            src = bank[:].rearrange("p j u r -> p j r u")
             if on_vector:
                 nc.vector.tensor_copy(out=words, in_=src)
             else:
                 nc.scalar.copy(out=words, in_=src)
 
-        def transpose_positions(c, a, part):
-            if c >= CHUNKS:
+        def turn_positions(h, part):
+            if h >= STEPS:
                 return
+            c, a = divmod(h, 2)
             n = CHUNK_PASSES[c]
-            if a == 0 and 0 in part:
+            if c not in y_grouped:
                 y_grouped[c] = stage.tile([P, n * BATCH * PACK], BF16, name="y_grouped", bufs=2, align_bytes=64)
-            words = y_next[c, a][:].bitcast(F32).rearrange("p u (s i) -> p u s i", i=P)
-            out_words = y_grouped[c][:].bitcast(F32).rearrange("p (s a r u) -> p s a r u", s=n, a=ROW_TILES, r=P)[:, :, a]
-            for s0 in part:
-                bank = banks.tile([P, 2, 2, P], F32, name="bank", tag="bank")
+            words = y_next[h][:].bitcast(F32).rearrange("p u (s i) -> p u s i", i=P)
+            grouped = y_grouped[c][:].bitcast(F32).rearrange("p (s a r u) -> p s a r u", s=n, a=ROW_TILES, r=P)
+            for s0 in [s for s in part if s % 2 == 0]:
+                bank = banks.tile([P, 2, PAIRS, P], F32, name="bank", tag="bank")
                 for s in range(2):
-                    for u in range(2):
+                    for u in range(PAIRS):
                         nc.tensor.transpose(bank[:, s, u, :], words[:, u, s0 + s, :], identity[:])
-                nc.scalar.copy(out=out_words[:, s0 : s0 + 2], in_=bank[:].rearrange("p s u r -> p s r u"))
+                copy_out(bank, grouped[:, s0 : s0 + 2, a], False)
 
-        def transpose_weights(piece, part, vec=()):
+        def turn_weights(piece, part, shared=False):
             n = piece[2]
-            if 0 in part:
-                w_grouped[piece] = stage.tile([P, n * GATES * PACK], BF16, name="w_grouped", bufs=3, align_bytes=64)
+            if piece not in w_grouped:
+                w_grouped[piece] = stage.tile([P, n * GATES * PACK], BF16, name="w_grouped", align_bytes=64)
+            grouped = w_grouped[piece][:].bitcast(F32).rearrange("p (s a r u) -> p s a r u", s=n, a=ROW_TILES, r=P)
             for s in part:
-                bank = new_bank()
+                bank = banks.tile([P, ROW_TILES, PAIRS, P], F32, name="bank", tag="bank")
                 for a in range(ROW_TILES):
-                    words = w_rows[piece][:, a, :].bitcast(F32)[:, s * 2 * P : (s + 1) * 2 * P]
-                    for u in range(PAIR_HALVES):
-                        nc.tensor.transpose(bank[:, a, u, :], words[:, u : 2 * P : 2], identity[:])
-                copy_out(bank, w_grouped[piece], s, n, s in vec)
+                    words = w_rows[piece][:, a, :].bitcast(F32)[:, s * PAIRS * P : (s + 1) * PAIRS * P]
+                    for u in range(PAIRS):
+                        nc.tensor.transpose(bank[:, a, u, :], words[:, u : PAIRS * P : PAIRS], identity[:])
+                copy_out(bank, grouped[:, s], shared and s % 2 == 1)
 
-        def quantise(grouped, columns, name, bufs):
-            codes = stage.tile([P, columns], U32, name=name + "_codes", align_bytes=64, bufs=bufs)
-            scales = stage.tile([P, columns], U8, name=name + "_scales", align_bytes=64, bufs=bufs)
+        def quantise(grouped, columns, name):
+            codes = stage.tile([P, columns], U32, name=name + "_codes", align_bytes=64, bufs=3)
+            scales = stage.tile([P, columns], U8, name=name + "_scales", align_bytes=64, bufs=3)
             nc.vector.quantize_mx(out=codes[:].bitcast(FP8X4), scales=scales[:], in_=grouped[:])
             return codes, scales
 
         def quantise_positions(c):
-            if c < CHUNKS:
-                y_codes[c] = quantise(y_grouped[c], CHUNK_PASSES[c] * BATCH, "y", 3)
+            y_codes[c] = quantise(y_grouped[c], CHUNK_PASSES[c] * BATCH, "y")
 
         def quantise_weights(piece):
-            w_codes[piece] = quantise(w_grouped[piece], piece[2] * GATES, "w", 3)
+            w_codes[piece] = quantise(w_grouped[piece], piece[2] * GATES, "w")
 
-        def multiply(c, piece, part=None):
-            which, first, n = piece
-            for a in range(ROW_TILES):
-                for s in range(n) if part is None else part:
-                    g = first + s
-                    n_cols = slice(s * GATES, (s + 1) * GATES)
+        def multiply(piece, part):
+            h, first, n = piece
+            c, which = divmod(h, 2)
+            for s in part:
+                g = first + s
+                n_cols = slice(s * GATES, (s + 1) * GATES)
+                for a in range(ROW_TILES):
                     m0 = ((g - FIRST_PASS[c]) * ROW_TILES + a) * P
-                    m_cols = slice(m0, m0 + P)
                     nc.tensor.matmul_mx(
                         out=acc[which, a][:],
-                        lhsT=y_codes[c][0][:, m_cols].bitcast(FP8X4),
-                        lhsT_scale=y_codes[c][1][:, m_cols],
+                        lhsT=y_codes[c][0][:, m0 : m0 + P].bitcast(FP8X4),
+                        lhsT_scale=y_codes[c][1][:, m0 : m0 + P],
                         rhs=w_codes[piece][0][:, n_cols].bitcast(FP8X4),
                         rhs_scale=w_codes[piece][1][:, n_cols],
                         start=(g == 0),
                         stop=(g == PASSES - 1),
                     )
 
-        LAST = CHUNKS - 1
         biased, gate = {}, {}
+        bias = consts.tile([P, 2 * GATES], F32, name="bias")
 
         def add_bias(which, a):
             biased[which, a] = finish.tile([P, GATES], F32, name="biased%d" % which)
             nc.vector.tensor_tensor(
-                out=biased[which, a][:], in0=acc[which, a][:], in1=bias[:, which * GATES : (which + 1) * GATES], op=ALU.add
+                out=biased[which, a][:],
+                in0=acc[which, a][:],
+                in1=bias[:, which * GATES : (which + 1) * GATES],
+                op=ALU.add,
             )
 
-        update_positions(0, 0)
-        transpose_positions(0, 0, range(0, CHUNK_PASSES[0], 2))
-        update_positions(0, 1)
-        for c in range(CHUNKS):
-            n = CHUNK_PASSES[c]
-            first_w, second_w = pieces(c, 0)[0], pieces(c, 1)
-            load_step(c + 3)
-            transpose_weights(first_w, range(0, n // 2))
-            transpose_positions(c, 1, range(0, n // 2, 2))
-            if c > 0:
-                last_w = pieces(c - 1, 1)[0]
-                multiply(c - 1, last_w, range(0, last_w[2] // 2))
-            transpose_positions(c, 1, range(n // 2, n, 2))
-            transpose_weights(first_w, range(n // 2, n))
-            if c > 0:
-                multiply(c - 1, last_w, range(last_w[2] // 2, last_w[2]))
-            update_positions(c + 1, 0)
-            quantise_positions(c)
+        queue, done = [], []
+
+        def multiply_next(keep):
+            while len(queue) - len(done) > keep:
+                multiply(*queue[len(done)])
+                done.append(None)
+
+        update_positions(0)
+        turn_positions(0, range(CHUNK_PASSES[0]))
+        update_positions(1)
+        for h in range(STEPS):
+            c = h // 2
+            load_step(h + 6)
+            last = h == STEPS - 1
+            first_w = pieces(h)[0]
+            w_halves = halves(first_w[2])
+            y_halves = halves(CHUNK_PASSES[(h + 1) // 2]) if not last else ((), ())
+            turn_weights(first_w, w_halves[0], last)
+            turn_positions(h + 1, y_halves[0])
+            multiply_next(2)
+            turn_positions(h + 1, y_halves[1])
+            turn_weights(first_w, w_halves[1], last)
+            multiply_next(1)
+            update_positions(h + 2)
+            if h % 2 == 0:
+                quantise_positions(c)
+            for piece in pieces(h)[1:]:
+                turn_weights(piece, range(piece[2]), True)
             quantise_weights(first_w)
-            if c < LAST:
-                more = CHUNK_PASSES[c + 1]
-                transpose_weights(second_w[0], range(0, n // 2))
-                transpose_positions(c + 1, 0, range(0, more // 2, 2))
-                multiply(c, first_w, range(0, n // 2))
-                transpose_positions(c + 1, 0, range(more // 2, more, 2))
-                transpose_weights(second_w[0], range(n // 2, n))
-                multiply(c, first_w, range(n // 2, n))
-                update_positions(c + 1, 1)
-                quantise_weights(second_w[0])
-            else:
-                for piece in second_w:
-                    transpose_weights(piece, range(piece[2]), (1,))
-                    pass
-                multiply(c, first_w)
-                for piece in second_w:
-                    quantise_weights(piece)
-                for a in range(ROW_TILES):
-                    add_bias(0, a)
-                    gate[a] = finish.tile([P, GATES], F32, name="gate")
-                    nc.scalar.activation(out=gate[a][:], in_=biased[0, a][:], func=ACT.Sigmoid)
-                for piece in second_w:
-                    multiply(c, piece)
-            if c == LAST - 2:
+            queue.extend((first_w, part) for part in w_halves)
+            for piece in pieces(h)[1:]:
+                quantise_weights(piece)
+                queue.append((piece, range(piece[2])))
+            if h == STEPS - 5:
                 bias_bank = banks.tile([P, 2 * GATES], F32, name="bias_bank", tag="bank")
                 nc.tensor.matmul(out=bias_bank[:], lhsT=ones[:], rhs=bias_row[:], start=True, stop=True)
-                bias = consts.tile([P, 2 * GATES], F32, name="bias")
                 nc.scalar.copy(out=bias[:], in_=bias_bank[:])
 
+        multiply_next(len(LAST_PIECES) + 1)
+        for a in range(ROW_TILES):
+            add_bias(0, a)
+            gate[a] = finish.tile([P, GATES], F32, name="gate")
+            nc.scalar.activation(out=gate[a][:], in_=biased[0, a][:], func=ACT.Sigmoid)
+        multiply_next(0)
         for a in range(ROW_TILES):
             add_bias(1, a)
             result = finish.tile([P, GATES], F32, name="result")

@@ -22,7 +22,7 @@ CHUNK_PASSES = (4, 4, 4, 4, 4, 4, 4, 4)
 CHUNKS = len(CHUNK_PASSES)
 FIRST_PASS = tuple(sum(CHUNK_PASSES[:c]) for c in range(CHUNKS))
 STEPS = 2 * CHUNKS
-LAST_PIECES = (2, 1, 1,)
+AHEAD = 5
 FLOPS = 2 * BATCH * MODES * 2 * GATES
 
 
@@ -36,8 +36,9 @@ def tile_instrumentedlocmblock_pb_k_kernel(
     nc = tc.nc
     with ExitStack() as ctx:
         consts = ctx.enter_context(tc.tile_pool(name="consts", bufs=1))
-        loads = ctx.enter_context(tc.tile_pool(name="loads", bufs=8))
+        loads = ctx.enter_context(tc.tile_pool(name="loads", bufs=7))
         stage = ctx.enter_context(tc.tile_pool(name="stage", bufs=3))
+        coded = ctx.enter_context(tc.tile_pool(name="coded", bufs=5))
         finish = ctx.enter_context(tc.tile_pool(name="finish", bufs=2))
         banks = ctx.enter_context(tc.psum_pool(name="banks", bufs=4))
         sums = ctx.enter_context(tc.psum_pool(name="sums", bufs=1))
@@ -52,35 +53,23 @@ def tile_instrumentedlocmblock_pb_k_kernel(
 
         y_rows, z_rows, w_rows = {}, {}, {}
 
-        def pieces(h):
-            c, which = divmod(h, 2)
-            sizes = LAST_PIECES if h == STEPS - 1 else (CHUNK_PASSES[c],)
-            return [(h, FIRST_PASS[c] + sum(sizes[:i]), n) for i, n in enumerate(sizes)]
-
-        def load_weights(h):
-            src = (glu_w1, glu_w2)[h % 2].rearrange("(a p) k -> p a k", p=P)
-            for piece in pieces(h):
-                first, n = piece[1:]
-                w_rows[piece] = loads.tile([P, ROW_TILES, n * K_PASS], BF16, name="w_rows", bufs=8)
-                nc.sync.dma_start(out=w_rows[piece][:], in_=src[:, :, first * K_PASS : (first + n) * K_PASS])
-
-        def load_positions(h):
-            if h >= STEPS:
-                return
-            c, a = divmod(h, 2)
-            cols = slice(FIRST_PASS[c] * K_PASS, (FIRST_PASS[c] + CHUNK_PASSES[c]) * K_PASS)
-            for src, name, keep in ((y_tilde, "y_rows", y_rows), (z_next, "z_rows", z_rows)):
-                keep[h] = loads.tile([P, CHUNK_PASSES[c] * K_PASS], BF16, name=name, bufs=8)
-                nc.sync.dma_start(out=keep[h][:], in_=src[a * P : (a + 1) * P, cols])
+        def modes_of(h):
+            first = FIRST_PASS[h // 2] * K_PASS
+            return slice(first, first + CHUNK_PASSES[h // 2] * K_PASS)
 
         def load_step(h):
             if h < STEPS:
-                load_weights(h)
-                load_positions(h + 2)
+                src = (glu_w1, glu_w2)[h % 2].rearrange("(a p) k -> p a k", p=P)
+                width = CHUNK_PASSES[h // 2] * K_PASS
+                w_rows[h] = loads.tile([P, ROW_TILES, width], BF16, name="w_rows")
+                nc.sync.dma_start(out=w_rows[h][:], in_=src[:, :, modes_of(h)])
+                rows = slice((h % 2) * P, (h % 2 + 1) * P)
+                y_rows[h] = loads.tile([P, width], BF16, name="y_rows")
+                nc.sync.dma_start(out=y_rows[h][:], in_=y_tilde[rows, modes_of(h)])
+                z_rows[h] = loads.tile([P, width], BF16, name="z_rows")
+                nc.sync.dma_start(out=z_rows[h][:], in_=z_next[rows, modes_of(h)])
 
-        load_positions(0)
-        load_positions(1)
-        for h in range(6):
+        for h in range(AHEAD):
             load_step(h)
 
         dt_f32 = consts.tile([P, 1], F32, name="dt_f32")
@@ -98,21 +87,23 @@ def tile_instrumentedlocmblock_pb_k_kernel(
 
         y_next, y_grouped, y_codes, w_grouped, w_codes = {}, {}, {}, {}, {}
 
-        def update_positions(h):
-            if h >= STEPS:
-                return
-            y_next[h] = stage.tile([P, PAIRS, CHUNK_PASSES[h // 2] * K_PASS // PAIRS], BF16, name="y_next", bufs=4)
-            for u in range(PAIRS):
-                nc.vector.scalar_tensor_tensor(
-                    out=y_next[h][:, u, :].rearrange("p (m e) -> p m e", e=2),
-                    in0=z_rows[h][:].rearrange("p (m u e) -> p u m e", u=PAIRS, e=2)[:, u],
-                    scalar=dt_f32[:, 0:1],
-                    in1=y_rows[h][:].rearrange("p (m u e) -> p u m e", u=PAIRS, e=2)[:, u],
-                    op0=ALU.mult,
-                    op1=ALU.add,
-                )
+        def update_positions(h, parts):
+            n = CHUNK_PASSES[h // 2]
+            y_next[h] = stage.tile([P, PAIRS, n * K_PASS // PAIRS], BF16, name="y_next")
+            split = "p (m u e) -> p u m e"
+            for part in parts:
+                pairs = slice(part.start * P, part.stop * P)
+                for u in range(PAIRS):
+                    nc.vector.scalar_tensor_tensor(
+                        out=y_next[h][:, u, :].rearrange("p (m e) -> p m e", e=2)[:, pairs],
+                        in0=z_rows[h][:].rearrange(split, u=PAIRS, e=2)[:, u, pairs],
+                        scalar=dt_f32[:, 0:1],
+                        in1=y_rows[h][:].rearrange(split, u=PAIRS, e=2)[:, u, pairs],
+                        op0=ALU.mult,
+                        op1=ALU.add,
+                    )
 
-        def copy_out(bank, words, on_vector):
+        def copy_out(bank, words, on_vector=False):
             src = bank[:].rearrange("p j u r -> p j r u")
             if on_vector:
                 nc.vector.tensor_copy(out=words, in_=src)
@@ -120,66 +111,106 @@ def tile_instrumentedlocmblock_pb_k_kernel(
                 nc.scalar.copy(out=words, in_=src)
 
         def turn_positions(h, part):
-            if h >= STEPS:
-                return
-            c, a = divmod(h, 2)
-            n = CHUNK_PASSES[c]
-            if c not in y_grouped:
-                y_grouped[c] = stage.tile([P, n * BATCH * PACK], BF16, name="y_grouped", bufs=2, align_bytes=64)
+            n = CHUNK_PASSES[h // 2]
+            if 0 in part:
+                y_grouped[h] = stage.tile([P, n * P * PACK], BF16, name="y_grouped", align_bytes=64)
             words = y_next[h][:].bitcast(F32).rearrange("p u (s i) -> p u s i", i=P)
-            grouped = y_grouped[c][:].bitcast(F32).rearrange("p (s a r u) -> p s a r u", s=n, a=ROW_TILES, r=P)
+            grouped = y_grouped[h][:].bitcast(F32).rearrange("p (s r u) -> p s r u", s=n, r=P)
             for s0 in [s for s in part if s % 2 == 0]:
                 bank = banks.tile([P, 2, PAIRS, P], F32, name="bank", tag="bank")
                 for s in range(2):
                     for u in range(PAIRS):
                         nc.tensor.transpose(bank[:, s, u, :], words[:, u, s0 + s, :], identity[:])
-                copy_out(bank, grouped[:, s0 : s0 + 2, a], False)
+                copy_out(bank, grouped[:, s0 : s0 + 2])
 
-        def turn_weights(piece, part, shared=False):
-            n = piece[2]
-            if piece not in w_grouped:
-                w_grouped[piece] = stage.tile([P, n * GATES * PACK], BF16, name="w_grouped", align_bytes=64)
-            grouped = w_grouped[piece][:].bitcast(F32).rearrange("p (s a r u) -> p s a r u", s=n, a=ROW_TILES, r=P)
+        def turn_weights(h, part):
+            n = CHUNK_PASSES[h // 2]
+            if 0 in part:
+                w_grouped[h] = stage.tile([P, n * GATES * PACK], BF16, name="w_grouped", align_bytes=64)
+            grouped = w_grouped[h][:].bitcast(F32).rearrange("p (s a r u) -> p s a r u", s=n, a=ROW_TILES, r=P)
             for s in part:
                 bank = banks.tile([P, ROW_TILES, PAIRS, P], F32, name="bank", tag="bank")
                 for a in range(ROW_TILES):
-                    words = w_rows[piece][:, a, :].bitcast(F32)[:, s * PAIRS * P : (s + 1) * PAIRS * P]
+                    words = w_rows[h][:, a, :].bitcast(F32)[:, s * PAIRS * P : (s + 1) * PAIRS * P]
                     for u in range(PAIRS):
                         nc.tensor.transpose(bank[:, a, u, :], words[:, u : PAIRS * P : PAIRS], identity[:])
-                copy_out(bank, grouped[:, s], shared and s % 2 == 1)
+                copy_out(bank, grouped[:, s])
 
         def quantise(grouped, columns, name):
-            codes = stage.tile([P, columns], U32, name=name + "_codes", align_bytes=64, bufs=3)
-            scales = stage.tile([P, columns], U8, name=name + "_scales", align_bytes=64, bufs=3)
+            codes = coded.tile([P, columns], U32, name=name + "_codes", align_bytes=64)
+            scales = coded.tile([P, columns], U8, name=name + "_scales", align_bytes=64)
             nc.vector.quantize_mx(out=codes[:].bitcast(FP8X4), scales=scales[:], in_=grouped[:])
             return codes, scales
 
-        def quantise_positions(c):
-            y_codes[c] = quantise(y_grouped[c], CHUNK_PASSES[c] * BATCH, "y")
+        def quantise_positions(h):
+            y_codes[h] = quantise(y_grouped[h], CHUNK_PASSES[h // 2] * P, "y")
 
-        def quantise_weights(piece):
-            w_codes[piece] = quantise(w_grouped[piece], piece[2] * GATES, "w")
+        def quantise_weights(h):
+            w_codes[h] = quantise(w_grouped[h], CHUNK_PASSES[h // 2] * GATES, "w")
 
-        def multiply(piece, part):
-            h, first, n = piece
-            c, which = divmod(h, 2)
-            for s in part:
-                g = first + s
+        def multiply(h, a):
+            codes, scales = y_codes[h - h % 2 + a]
+            for s in range(CHUNK_PASSES[h // 2]):
+                g = FIRST_PASS[h // 2] + s
+                m_cols = slice(s * P, (s + 1) * P)
                 n_cols = slice(s * GATES, (s + 1) * GATES)
-                for a in range(ROW_TILES):
-                    m0 = ((g - FIRST_PASS[c]) * ROW_TILES + a) * P
-                    nc.tensor.matmul_mx(
-                        out=acc[which, a][:],
-                        lhsT=y_codes[c][0][:, m0 : m0 + P].bitcast(FP8X4),
-                        lhsT_scale=y_codes[c][1][:, m0 : m0 + P],
-                        rhs=w_codes[piece][0][:, n_cols].bitcast(FP8X4),
-                        rhs_scale=w_codes[piece][1][:, n_cols],
-                        start=(g == 0),
-                        stop=(g == PASSES - 1),
-                    )
+                nc.tensor.matmul_mx(
+                    out=acc[h % 2, a][:],
+                    lhsT=codes[:, m_cols].bitcast(FP8X4),
+                    lhsT_scale=scales[:, m_cols],
+                    rhs=w_codes[h][0][:, n_cols].bitcast(FP8X4),
+                    rhs_scale=w_codes[h][1][:, n_cols],
+                    start=(g == 0),
+                    stop=(g == PASSES - 1),
+                )
+
+        bias = consts.tile([P, 2 * GATES], F32, name="bias")
+
+        def spread_bias():
+            bias_bank = banks.tile([P, 2 * GATES], F32, name="bias_bank", tag="bank")
+            nc.tensor.matmul(out=bias_bank[:], lhsT=ones[:], rhs=bias_row[:], start=True, stop=True)
+            nc.scalar.copy(out=bias[:], in_=bias_bank[:])
+
+        groups = {}
+        for c in range(CHUNKS):
+            for a in range(ROW_TILES):
+                groups[2 * c + a + 3] = [(2 * c, a), (2 * c + 1, a)]
+
+        for h in range(STEPS):
+            load_step(h + AHEAD)
+            n_halves = halves(CHUNK_PASSES[h // 2])
+            ready = groups.get(h, [])
+            if h > 0:
+                before = halves(CHUNK_PASSES[(h - 1) // 2])
+                update_positions(h - 1, before if h == 1 else [range(0, CHUNK_PASSES[(h - 1) // 2])])
+            turn_weights(h, n_halves[0])
+            if h > 0:
+                turn_positions(h - 1, before[0])
+            for group in ready[:1]:
+                multiply(*group)
+            if h > 0:
+                turn_positions(h - 1, before[1])
+            turn_weights(h, n_halves[1])
+            for group in ready[1:]:
+                multiply(*group)
+            if h > 1:
+                quantise_positions(h - 2)
+            if h > 0:
+                quantise_weights(h - 1)
+            if h == 2:
+                spread_bias()
+
+        final = STEPS - 1
+        update_positions(final, halves(CHUNK_PASSES[-1]))
+        quantise_positions(final - 1)
+        quantise_weights(final)
+        turn_positions(final, range(0, CHUNK_PASSES[-1]))
+        for h in range(STEPS, max(groups)):
+            for group in groups.get(h, []):
+                multiply(*group)
+        quantise_positions(final)
 
         biased, gate = {}, {}
-        bias = consts.tile([P, 2 * GATES], F32, name="bias")
 
         def add_bias(which, a):
             biased[which, a] = finish.tile([P, GATES], F32, name="biased%d" % which)
@@ -189,53 +220,20 @@ def tile_instrumentedlocmblock_pb_k_kernel(
                 in1=bias[:, which * GATES : (which + 1) * GATES],
                 op=ALU.add,
             )
+            if which == 0:
+                gate[a] = finish.tile([P, GATES], F32, name="gate")
+                nc.scalar.activation(out=gate[a][:], in_=biased[0, a][:], func=ACT.Sigmoid)
 
-        queue, done = [], []
-
-        def multiply_next(keep):
-            while len(queue) - len(done) > keep:
-                multiply(*queue[len(done)])
-                done.append(None)
-
-        update_positions(0)
-        turn_positions(0, range(CHUNK_PASSES[0]))
-        update_positions(1)
-        for h in range(STEPS):
-            c = h // 2
-            load_step(h + 6)
-            last = h == STEPS - 1
-            first_w = pieces(h)[0]
-            w_halves = halves(first_w[2])
-            y_halves = halves(CHUNK_PASSES[(h + 1) // 2]) if not last else ((), ())
-            turn_weights(first_w, w_halves[0], last)
-            turn_positions(h + 1, y_halves[0])
-            multiply_next(2)
-            turn_positions(h + 1, y_halves[1])
-            turn_weights(first_w, w_halves[1], last)
-            multiply_next(1)
-            update_positions(h + 2)
-            if h % 2 == 0:
-                quantise_positions(c)
-            for piece in pieces(h)[1:]:
-                turn_weights(piece, range(piece[2]), True)
-            quantise_weights(first_w)
-            queue.extend((first_w, part) for part in w_halves)
-            for piece in pieces(h)[1:]:
-                quantise_weights(piece)
-                queue.append((piece, range(piece[2])))
-            if h == STEPS - 5:
-                bias_bank = banks.tile([P, 2 * GATES], F32, name="bias_bank", tag="bank")
-                nc.tensor.matmul(out=bias_bank[:], lhsT=ones[:], rhs=bias_row[:], start=True, stop=True)
-                nc.scalar.copy(out=bias[:], in_=bias_bank[:])
-
-        multiply_next(len(LAST_PIECES) + 1)
-        for a in range(ROW_TILES):
-            add_bias(0, a)
-            gate[a] = finish.tile([P, GATES], F32, name="gate")
-            nc.scalar.activation(out=gate[a][:], in_=biased[0, a][:], func=ACT.Sigmoid)
-        multiply_next(0)
-        for a in range(ROW_TILES):
-            add_bias(1, a)
+        def store_rows(a):
             result = finish.tile([P, GATES], F32, name="result")
             nc.vector.tensor_mul(out=result[:], in0=gate[a][:], in1=biased[1, a][:])
             nc.sync.dma_start(out=out[a * P : (a + 1) * P, :], in_=result[:])
+
+        add_bias(0, 0)
+        add_bias(1, 0)
+        for group in groups[max(groups)]:
+            multiply(*group)
+        add_bias(0, 1)
+        store_rows(0)
+        add_bias(1, 1)
+        store_rows(1)

@@ -22,12 +22,13 @@ CHUNK_PASSES = (4, 4, 4, 4, 4, 4, 4, 4)
 CHUNKS = len(CHUNK_PASSES)
 FIRST_PASS = tuple(sum(CHUNK_PASSES[:c]) for c in range(CHUNKS))
 STEPS = 2 * CHUNKS
+WIDEST = 1024
 AHEAD = 5
 FLOPS = 2 * BATCH * MODES * 2 * GATES
 
 
-def halves(n):
-    return range(0, n // 2), range(n // 2, n)
+def pairs_of(n):
+    return [range(s, min(s + 2, n)) for s in range(0, n, 2)]
 
 
 def tile_instrumentedlocmblock_pb_k_kernel(
@@ -44,8 +45,11 @@ def tile_instrumentedlocmblock_pb_k_kernel(
         sums = ctx.enter_context(tc.psum_pool(name="sums", bufs=1))
         ctx.enter_context(tc.manual_schedule())
 
-        dt_bf16 = consts.tile([P, 1], BF16, name="dt_bf16")
-        nc.scalar.dma_start(out=dt_bf16[:], in_=dt.partition_broadcast(P))
+        dt_row = consts.tile([P, 2], BF16, name="dt_row")
+        nc.vector.memset(dt_row[:], 0.0)
+        nc.scalar.dma_start(out=dt_row[0:1, 0:1], in_=dt.unsqueeze(0))
+        ones = consts.tile([P, P], BF16, name="ones")
+        nc.vector.memset(ones[:], 1.0)
         bias_row = consts.tile([P, 2 * GATES], BF16, name="bias_row")
         nc.vector.memset(bias_row[:], 0.0)
         nc.scalar.dma_start(out=bias_row[0:1, 0:GATES], in_=glu_b1.unsqueeze(0))
@@ -57,29 +61,36 @@ def tile_instrumentedlocmblock_pb_k_kernel(
             first = FIRST_PASS[h // 2] * K_PASS
             return slice(first, first + CHUNK_PASSES[h // 2] * K_PASS)
 
+        def load_positions(h):
+            width = CHUNK_PASSES[h // 2] * K_PASS
+            rows = slice((h % 2) * P, (h % 2 + 1) * P)
+            y_rows[h] = loads.tile([P, width], BF16, name="y_rows")
+            nc.sync.dma_start(out=y_rows[h][:], in_=y_tilde[rows, modes_of(h)])
+            z_rows[h] = loads.tile([P, width], BF16, name="z_rows")
+            nc.sync.dma_start(out=z_rows[h][:], in_=z_next[rows, modes_of(h)])
+
         def load_step(h):
             if h < STEPS:
+                if h == 0:
+                    load_positions(h)
                 src = (glu_w1, glu_w2)[h % 2].rearrange("(a p) k -> p a k", p=P)
                 width = CHUNK_PASSES[h // 2] * K_PASS
                 w_rows[h] = loads.tile([P, ROW_TILES, width], BF16, name="w_rows")
                 nc.sync.dma_start(out=w_rows[h][:], in_=src[:, :, modes_of(h)])
-                rows = slice((h % 2) * P, (h % 2 + 1) * P)
-                y_rows[h] = loads.tile([P, width], BF16, name="y_rows")
-                nc.sync.dma_start(out=y_rows[h][:], in_=y_tilde[rows, modes_of(h)])
-                z_rows[h] = loads.tile([P, width], BF16, name="z_rows")
-                nc.sync.dma_start(out=z_rows[h][:], in_=z_next[rows, modes_of(h)])
+                if h > 0:
+                    load_positions(h)
 
         for h in range(AHEAD):
             load_step(h)
 
-        dt_f32 = consts.tile([P, 1], F32, name="dt_f32")
-        nc.vector.tensor_copy(out=dt_f32[:], in_=dt_bf16[:])
+        dt_bank = banks.tile([P, 2], F32, name="dt_bank", tag="bank")
+        nc.tensor.matmul(out=dt_bank[:], lhsT=ones[:], rhs=dt_row[:], start=True, stop=True)
+        dt_f32 = consts.tile([P, 2], F32, name="dt_f32")
+        nc.vector.tensor_copy(out=dt_f32[:], in_=dt_bank[:])
         identity = consts.tile([P, P], F32, name="identity")
         make_identity(nc, identity[:])
-        ones = consts.tile([P, P], BF16, name="ones")
-        nc.vector.memset(ones[:], 1.0)
         table_warmer = consts.tile([P, 1], F32, name="table_warmer")
-        nc.scalar.activation(out=table_warmer[:], in_=dt_f32[:], func=ACT.Sigmoid)
+        nc.scalar.activation(out=table_warmer[:], in_=ones[:, 0:1], func=ACT.Sigmoid)
         acc = {}
         for which in range(2):
             for a in range(ROW_TILES):
@@ -139,7 +150,10 @@ def tile_instrumentedlocmblock_pb_k_kernel(
         def quantise(grouped, columns, name):
             codes = coded.tile([P, columns], U32, name=name + "_codes", align_bytes=64)
             scales = coded.tile([P, columns], U8, name=name + "_scales", align_bytes=64)
-            nc.vector.quantize_mx(out=codes[:].bitcast(FP8X4), scales=scales[:], in_=grouped[:])
+            for first in range(0, columns, WIDEST):
+                part = slice(first, min(first + WIDEST, columns))
+                words = slice(part.start * PACK, part.stop * PACK)
+                nc.vector.quantize_mx(out=codes[:, part].bitcast(FP8X4), scales=scales[:, part], in_=grouped[:, words])
             return codes, scales
 
         def quantise_positions(h):
@@ -148,9 +162,9 @@ def tile_instrumentedlocmblock_pb_k_kernel(
         def quantise_weights(h):
             w_codes[h] = quantise(w_grouped[h], CHUNK_PASSES[h // 2] * GATES, "w")
 
-        def multiply(h, a):
+        def multiply(h, a, part):
             codes, scales = y_codes[h - h % 2 + a]
-            for s in range(CHUNK_PASSES[h // 2]):
+            for s in part:
                 g = FIRST_PASS[h // 2] + s
                 m_cols = slice(s * P, (s + 1) * P)
                 n_cols = slice(s * GATES, (s + 1) * GATES)
@@ -171,43 +185,50 @@ def tile_instrumentedlocmblock_pb_k_kernel(
             nc.tensor.matmul(out=bias_bank[:], lhsT=ones[:], rhs=bias_row[:], start=True, stop=True)
             nc.scalar.copy(out=bias[:], in_=bias_bank[:])
 
-        groups = {}
-        for c in range(CHUNKS):
-            for a in range(ROW_TILES):
-                groups[2 * c + a + 3] = [(2 * c, a), (2 * c + 1, a)]
+        queue, done = [], []
+
+        def add_groups(c, a):
+            for h in (2 * c, 2 * c + 1):
+                queue.extend((h, a, part) for part in pairs_of(CHUNK_PASSES[c]))
+
+        def multiply_next(count):
+            for i in range(count):
+                multiply(*queue[len(done)])
+                done.append(None)
 
         for h in range(STEPS):
             load_step(h + AHEAD)
-            n_halves = halves(CHUNK_PASSES[h // 2])
-            ready = groups.get(h, [])
+            w_pairs = pairs_of(CHUNK_PASSES[h // 2])
+            y_pairs = []
             if h > 0:
-                before = halves(CHUNK_PASSES[(h - 1) // 2])
-                update_positions(h - 1, before if h == 1 else [range(0, CHUNK_PASSES[(h - 1) // 2])])
-            turn_weights(h, n_halves[0])
-            if h > 0:
-                turn_positions(h - 1, before[0])
-            for group in ready[:1]:
-                multiply(*group)
-            if h > 0:
-                turn_positions(h - 1, before[1])
-            turn_weights(h, n_halves[1])
-            for group in ready[1:]:
-                multiply(*group)
+                y_pairs = pairs_of(CHUNK_PASSES[(h - 1) // 2])
+                update_positions(h - 1, y_pairs if h == 1 else [range(0, CHUNK_PASSES[(h - 1) // 2])])
             if h > 1:
                 quantise_positions(h - 2)
             if h > 0:
                 quantise_weights(h - 1)
+            if h > 1:
+                add_groups((h - 2) // 2, h % 2)
+            for i in range(max(len(w_pairs), len(y_pairs))):
+                if i < len(w_pairs) and i % 2 == 0:
+                    turn_weights(h, w_pairs[i])
+                if i < len(y_pairs):
+                    turn_positions(h - 1, y_pairs[i])
+                if i < len(w_pairs) and i % 2 == 1:
+                    turn_weights(h, w_pairs[i])
+                multiply_next(min(2, max(0, len(queue) - len(done) - 2)))
             if h == 2:
                 spread_bias()
 
         final = STEPS - 1
-        update_positions(final, halves(CHUNK_PASSES[-1]))
+        update_positions(final, pairs_of(CHUNK_PASSES[-1]))
         quantise_positions(final - 1)
         quantise_weights(final)
-        turn_positions(final, range(0, CHUNK_PASSES[-1]))
-        for h in range(STEPS, max(groups)):
-            for group in groups.get(h, []):
-                multiply(*group)
+        add_groups(CHUNKS - 1, 0)
+
+        for part in pairs_of(CHUNK_PASSES[-1]):
+            turn_positions(final, part)
+        multiply_next(len(queue) - len(done))
         quantise_positions(final)
 
         biased, gate = {}, {}
@@ -231,8 +252,8 @@ def tile_instrumentedlocmblock_pb_k_kernel(
 
         add_bias(0, 0)
         add_bias(1, 0)
-        for group in groups[max(groups)]:
-            multiply(*group)
+        add_groups(CHUNKS - 1, 1)
+        multiply_next(len(queue) - len(done))
         add_bias(0, 1)
         store_rows(0)
         add_bias(1, 1)

@@ -18,12 +18,11 @@ K_PASS = P * PACK
 PASSES = MODES // K_PASS
 ROW_TILES = 2
 PAIRS = 2
-CHUNK_PASSES = (4, 4, 4, 4, 4, 4, 4, 4)
+CHUNK_PASSES = (6, 6, 6, 6, 4, 4)
 CHUNKS = len(CHUNK_PASSES)
 FIRST_PASS = tuple(sum(CHUNK_PASSES[:c]) for c in range(CHUNKS))
 STEPS = 2 * CHUNKS
-WIDEST = 1024
-AHEAD = 5
+AHEAD = 3
 FLOPS = 2 * BATCH * MODES * 2 * GATES
 
 
@@ -37,9 +36,9 @@ def tile_instrumentedlocmblock_pb_k_kernel(
     nc = tc.nc
     with ExitStack() as ctx:
         consts = ctx.enter_context(tc.tile_pool(name="consts", bufs=1))
-        loads = ctx.enter_context(tc.tile_pool(name="loads", bufs=7))
+        loads = ctx.enter_context(tc.tile_pool(name="loads", bufs=4))
         stage = ctx.enter_context(tc.tile_pool(name="stage", bufs=3))
-        coded = ctx.enter_context(tc.tile_pool(name="coded", bufs=5))
+        coded = ctx.enter_context(tc.tile_pool(name="coded", bufs=4))
         finish = ctx.enter_context(tc.tile_pool(name="finish", bufs=2))
         banks = ctx.enter_context(tc.psum_pool(name="banks", bufs=4))
         sums = ctx.enter_context(tc.psum_pool(name="sums", bufs=1))
@@ -147,20 +146,19 @@ def tile_instrumentedlocmblock_pb_k_kernel(
                         nc.tensor.transpose(bank[:, a, u, :], words[:, u : PAIRS * P : PAIRS], identity[:])
                 copy_out(bank, grouped[:, s])
 
-        def quantise(grouped, columns, name):
+        def quantise(grouped, columns, name, unit):
             codes = coded.tile([P, columns], U32, name=name + "_codes", align_bytes=64)
             scales = coded.tile([P, columns], U8, name=name + "_scales", align_bytes=64)
-            for first in range(0, columns, WIDEST):
-                part = slice(first, min(first + WIDEST, columns))
+            for part in [slice(f, min(f + 4 * unit, columns)) for f in range(0, columns, 4 * unit)]:
                 words = slice(part.start * PACK, part.stop * PACK)
                 nc.vector.quantize_mx(out=codes[:, part].bitcast(FP8X4), scales=scales[:, part], in_=grouped[:, words])
             return codes, scales
 
         def quantise_positions(h):
-            y_codes[h] = quantise(y_grouped[h], CHUNK_PASSES[h // 2] * P, "y")
+            y_codes[h] = quantise(y_grouped[h], CHUNK_PASSES[h // 2] * P, "y", P)
 
         def quantise_weights(h):
-            w_codes[h] = quantise(w_grouped[h], CHUNK_PASSES[h // 2] * GATES, "w")
+            w_codes[h] = quantise(w_grouped[h], CHUNK_PASSES[h // 2] * GATES, "w", GATES)
 
         def multiply(h, a, part):
             codes, scales = y_codes[h - h % 2 + a]

from contextlib import ExitStack

import concourse.mybir as mybir
from concourse.masks import make_identity

BF16 = mybir.dt.bfloat16
F32 = mybir.dt.float32
U32 = mybir.dt.uint32
U8 = mybir.dt.uint8
FP8X4 = mybir.dt.float8_e4m3fn_x4
ALU = mybir.AluOpType
ACT = mybir.ActivationFunctionType

BATCH, MODES, GATES = 256, 16384, 256
P = 128
PACK = 4
K_PASS = P * PACK
PASSES = MODES // K_PASS
ROW_TILES = 2
PAIRS = 2
CHUNK_PASSES = (6, 6, 6, 6, 4, 4)
CHUNKS = len(CHUNK_PASSES)
FIRST_PASS = tuple(sum(CHUNK_PASSES[:c]) for c in range(CHUNKS))
STEPS = 2 * CHUNKS
AHEAD = 3
FLOPS = 2 * BATCH * MODES * 2 * GATES


def pairs_of(n):
    return [range(s, min(s + 2, n)) for s in range(0, n, 2)]


def tile_instrumentedlocmblock_pb_k_kernel(
    tc, y_tilde, z_next, dt, glu_w1, glu_w2, glu_b1, glu_b2, out
):
    nc = tc.nc
    with ExitStack() as ctx:
        consts = ctx.enter_context(tc.tile_pool(name="consts", bufs=1))
        loads = ctx.enter_context(tc.tile_pool(name="loads", bufs=4))
        stage = ctx.enter_context(tc.tile_pool(name="stage", bufs=3))
        coded = ctx.enter_context(tc.tile_pool(name="coded", bufs=4))
        finish = ctx.enter_context(tc.tile_pool(name="finish", bufs=2))
        banks = ctx.enter_context(tc.psum_pool(name="banks", bufs=4))
        sums = ctx.enter_context(tc.psum_pool(name="sums", bufs=1))
        ctx.enter_context(tc.manual_schedule())

        dt_row = consts.tile([P, 2], BF16, name="dt_row")
        nc.vector.memset(dt_row[:], 0.0)
        nc.scalar.dma_start(out=dt_row[0:1, 0:1], in_=dt.unsqueeze(0))
        ones = consts.tile([P, P], BF16, name="ones")
        nc.vector.memset(ones[:], 1.0)
        bias_row = consts.tile([P, 2 * GATES], BF16, name="bias_row")
        nc.vector.memset(bias_row[:], 0.0)
        nc.scalar.dma_start(out=bias_row[0:1, 0:GATES], in_=glu_b1.unsqueeze(0))
        nc.scalar.dma_start(out=bias_row[0:1, GATES:], in_=glu_b2.unsqueeze(0))

        y_rows, z_rows, w_rows = {}, {}, {}

        def modes_of(h):
            first = FIRST_PASS[h // 2] * K_PASS
            return slice(first, first + CHUNK_PASSES[h // 2] * K_PASS)

        def load_positions(h):
            width = CHUNK_PASSES[h // 2] * K_PASS
            rows = slice((h % 2) * P, (h % 2 + 1) * P)
            y_rows[h] = loads.tile([P, width], BF16, name="y_rows")
            nc.sync.dma_start(out=y_rows[h][:], in_=y_tilde[rows, modes_of(h)])
            z_rows[h] = loads.tile([P, width], BF16, name="z_rows")
            nc.sync.dma_start(out=z_rows[h][:], in_=z_next[rows, modes_of(h)])

        def load_step(h):
            if h < STEPS:
                if h == 0:
                    load_positions(h)
                src = (glu_w1, glu_w2)[h % 2].rearrange("(a p) k -> p a k", p=P)
                width = CHUNK_PASSES[h // 2] * K_PASS
                w_rows[h] = loads.tile([P, ROW_TILES, width], BF16, name="w_rows")
                nc.sync.dma_start(out=w_rows[h][:], in_=src[:, :, modes_of(h)])
                if h > 0:
                    load_positions(h)

        for h in range(AHEAD):
            load_step(h)

        dt_bank = banks.tile([P, 2], F32, name="dt_bank", tag="bank")
        nc.tensor.matmul(out=dt_bank[:], lhsT=ones[:], rhs=dt_row[:], start=True, stop=True)
        dt_f32 = consts.tile([P, 2], F32, name="dt_f32")
        nc.vector.tensor_copy(out=dt_f32[:], in_=dt_bank[:])
        identity = consts.tile([P, P], F32, name="identity")
        make_identity(nc, identity[:])
        table_warmer = consts.tile([P, 1], F32, name="table_warmer")
        nc.scalar.activation(out=table_warmer[:], in_=ones[:, 0:1], func=ACT.Sigmoid)
        acc = {}
        for which in range(2):
            for a in range(ROW_TILES):
                acc[which, a] = sums.tile([P, GATES], F32, name="acc%d%d" % (which, a))

        y_next, y_grouped, y_codes, w_grouped, w_codes = {}, {}, {}, {}, {}

        def update_positions(h, parts):
            n = CHUNK_PASSES[h // 2]
            y_next[h] = stage.tile([P, PAIRS, n * K_PASS // PAIRS], BF16, name="y_next")
            split = "p (m u e) -> p u m e"
            for part in parts:
                pairs = slice(part.start * P, part.stop * P)
                for u in range(PAIRS):
                    nc.vector.scalar_tensor_tensor(
                        out=y_next[h][:, u, :].rearrange("p (m e) -> p m e", e=2)[:, pairs],
                        in0=z_rows[h][:].rearrange(split, u=PAIRS, e=2)[:, u, pairs],
                        scalar=dt_f32[:, 0:1],
                        in1=y_rows[h][:].rearrange(split, u=PAIRS, e=2)[:, u, pairs],
                        op0=ALU.mult,
                        op1=ALU.add,
                    )

        def copy_out(bank, words, on_vector=False):
            src = bank[:].rearrange("p j u r -> p j r u")
            if on_vector:
                nc.vector.tensor_copy(out=words, in_=src)
            else:
                nc.scalar.copy(out=words, in_=src)

        def turn_positions(h, part):
            n = CHUNK_PASSES[h // 2]
            if 0 in part:
                y_grouped[h] = stage.tile([P, n * P * PACK], BF16, name="y_grouped", align_bytes=64)
            words = y_next[h][:].bitcast(F32).rearrange("p u (s i) -> p u s i", i=P)
            grouped = y_grouped[h][:].bitcast(F32).rearrange("p (s r u) -> p s r u", s=n, r=P)
            for s0 in [s for s in part if s % 2 == 0]:
                bank = banks.tile([P, 2, PAIRS, P], F32, name="bank", tag="bank")
                for s in range(2):
                    for u in range(PAIRS):
                        nc.tensor.transpose(bank[:, s, u, :], words[:, u, s0 + s, :], identity[:])
                copy_out(bank, grouped[:, s0 : s0 + 2])

        def turn_weights(h, part):
            n = CHUNK_PASSES[h // 2]
            if 0 in part:
                w_grouped[h] = stage.tile([P, n * GATES * PACK], BF16, name="w_grouped", align_bytes=64)
            grouped = w_grouped[h][:].bitcast(F32).rearrange("p (s a r u) -> p s a r u", s=n, a=ROW_TILES, r=P)
            for s in part:
                bank = banks.tile([P, ROW_TILES, PAIRS, P], F32, name="bank", tag="bank")
                for a in range(ROW_TILES):
                    words = w_rows[h][:, a, :].bitcast(F32)[:, s * PAIRS * P : (s + 1) * PAIRS * P]
                    for u in range(PAIRS):
                        nc.tensor.transpose(bank[:, a, u, :], words[:, u : PAIRS * P : PAIRS], identity[:])
                copy_out(bank, grouped[:, s])

        def quantise(grouped, columns, name, unit):
            codes = coded.tile([P, columns], U32, name=name + "_codes", align_bytes=64)
            scales = coded.tile([P, columns], U8, name=name + "_scales", align_bytes=64)
            for part in [slice(f, min(f + 4 * unit, columns)) for f in range(0, columns, 4 * unit)]:
                words = slice(part.start * PACK, part.stop * PACK)
                nc.vector.quantize_mx(out=codes[:, part].bitcast(FP8X4), scales=scales[:, part], in_=grouped[:, words])
            return codes, scales

        def quantise_positions(h):
            y_codes[h] = quantise(y_grouped[h], CHUNK_PASSES[h // 2] * P, "y", P)

        def quantise_weights(h):
            w_codes[h] = quantise(w_grouped[h], CHUNK_PASSES[h // 2] * GATES, "w", GATES)

        def multiply(h, a, part):
            codes, scales = y_codes[h - h % 2 + a]
            for s in part:
                g = FIRST_PASS[h // 2] + s
                m_cols = slice(s * P, (s + 1) * P)
                n_cols = slice(s * GATES, (s + 1) * GATES)
                nc.tensor.matmul_mx(
                    out=acc[h % 2, a][:],
                    lhsT=codes[:, m_cols].bitcast(FP8X4),
                    lhsT_scale=scales[:, m_cols],
                    rhs=w_codes[h][0][:, n_cols].bitcast(FP8X4),
                    rhs_scale=w_codes[h][1][:, n_cols],
                    start=(g == 0),
                    stop=(g == PASSES - 1),
                )

        bias = consts.tile([P, 2 * GATES], F32, name="bias")

        def spread_bias():
            bias_bank = banks.tile([P, 2 * GATES], F32, name="bias_bank", tag="bank")
            nc.tensor.matmul(out=bias_bank[:], lhsT=ones[:], rhs=bias_row[:], start=True, stop=True)
            nc.scalar.copy(out=bias[:], in_=bias_bank[:])

        queue, done = [], []

        def add_groups(c, a):
            for h in (2 * c, 2 * c + 1):
                queue.extend((h, a, part) for part in pairs_of(CHUNK_PASSES[c]))

        def multiply_next(count):
            for i in range(count):
                multiply(*queue[len(done)])
                done.append(None)

        for h in range(STEPS):
            load_step(h + AHEAD)
            w_pairs = pairs_of(CHUNK_PASSES[h // 2])
            y_pairs = []
            if h > 0:
                y_pairs = pairs_of(CHUNK_PASSES[(h - 1) // 2])
                update_positions(h - 1, y_pairs if h == 1 else [range(0, CHUNK_PASSES[(h - 1) // 2])])
            if h > 1:
                quantise_positions(h - 2)
            if h > 0:
                quantise_weights(h - 1)
            if h > 1:
                add_groups((h - 2) // 2, h % 2)
            for i in range(max(len(w_pairs), len(y_pairs))):
                if i < len(w_pairs) and i % 2 == 0:
                    turn_weights(h, w_pairs[i])
                if i < len(y_pairs):
                    turn_positions(h - 1, y_pairs[i])
                if i < len(w_pairs) and i % 2 == 1:
                    turn_weights(h, w_pairs[i])
                multiply_next(min(2, max(0, len(queue) - len(done) - 2)))
            if h == 2:
                spread_bias()

        final = STEPS - 1
        update_positions(final, pairs_of(CHUNK_PASSES[-1]))
        quantise_positions(final - 1)
        quantise_weights(final)
        add_groups(CHUNKS - 1, 0)

        for part in pairs_of(CHUNK_PASSES[-1]):
            turn_positions(final, part)
        multiply_next(len(queue) - len(done))
        quantise_positions(final)

        biased, gate = {}, {}

        def add_bias(which, a):
            biased[which, a] = finish.tile([P, GATES], F32, name="biased%d" % which)
            nc.vector.tensor_tensor(
                out=biased[which, a][:],
                in0=acc[which, a][:],
                in1=bias[:, which * GATES : (which + 1) * GATES],
                op=ALU.add,
            )
            if which == 0:
                gate[a] = finish.tile([P, GATES], F32, name="gate")
                nc.scalar.activation(out=gate[a][:], in_=biased[0, a][:], func=ACT.Sigmoid)

        def store_rows(a):
            result = finish.tile([P, GATES], F32, name="result")
            nc.vector.tensor_mul(out=result[:], in0=gate[a][:], in1=biased[1, a][:])
            nc.sync.dma_start(out=out[a * P : (a + 1) * P, :], in_=result[:])

        add_bias(0, 0)
        add_bias(1, 0)
        add_groups(CHUNKS - 1, 1)
        multiply_next(len(queue) - len(done))
        add_bias(0, 1)
        store_rows(0)
        add_bias(1, 1)
        store_rows(1)
